import numpy as np
import ml_dtypes


def mxq(x, axis, fmt="e4m3"):
    dtype, down = {"e4m3": (ml_dtypes.float8_e4m3fn, 7), "e5m2": (ml_dtypes.float8_e5m2, 14)}[fmt]
    v = np.moveaxis(np.asarray(x, np.float32).astype(ml_dtypes.bfloat16).astype(np.float64), axis, -1)
    blocks = v.reshape(v.shape[:-1] + (-1, 32))
    amax = np.abs(blocks).max(-1, keepdims=True)
    byte = np.maximum(np.where(amax > 0, np.frexp(amax)[1] - 1 + 127, 0) - down, 1)
    scale = np.exp2(byte - 127.0)
    codes = (blocks / scale).astype(np.float32).astype(dtype).astype(np.float64)
    return np.moveaxis((codes * scale).reshape(v.shape), -1, axis)


WIDE = False


def mx_kscale(k):
    if not WIDE:
        return np.ones(k)
    levels = np.array([10, -10, 5, -5, 0])
    a = np.random.permutation(np.resize(levels, k // 512 * 4)).reshape(k // 512, 4)
    idx = np.arange(k)
    return np.exp2(a[idx // 512, idx % 128 // 32])


BF16 = ml_dtypes.bfloat16


def bf(x):
    return np.asarray(x, np.float32).astype(BF16)


def f64(x):
    return np.asarray(x).astype(np.float64)


B, C, HH, WW, M, L, G, HID = 4, 1536, 32, 32, 128, 512, 256, 512
N = HH * WW
ITERS = 3
DUST = 1.0


def lse(a, axis):
    top = a.max(axis=axis, keepdims=True)
    return np.log(np.exp(a - top).sum(axis=axis)) + np.squeeze(top, axis=axis)


def setup_inputs():
    s, t = mx_kscale(C), mx_kscale(HID)
    return {
        "x": bf(np.random.standard_normal((B, C, HH, WW)) * s[None, :, None, None]),
        "Ws1": bf(np.random.standard_normal((HID, C)) / np.sqrt(C) / s[None, :] * t[:, None]),
        "bs1": bf(np.random.standard_normal(HID) * 0.3 * t),
        "Ws2": bf(np.random.standard_normal((M, HID)) * 2.0 / np.sqrt(HID) / t[None, :]),
    }


def reference(x, Ws1, bs1, Ws2):
    xf = f64(x).reshape(B, C, N)
    hs = np.maximum((mxq(f64(Ws1), 1, "e4m3") @ mxq(xf, 1, "e4m3")) + f64(bs1)[None, :, None], 0.0)
    p = mxq(f64(Ws2), 1, "e4m3") @ mxq(hs, 1, "e4m3")
    norm = -np.log(M + N)
    log_mu = np.concatenate([np.full(M, norm), np.full(1, np.log(N) + norm)])
    log_nu = np.full(N, norm)
    Z = np.concatenate([p, np.full((B, 1, N), DUST)], axis=1)
    u = np.zeros((B, M + 1))
    v = np.zeros((B, N))
    for _ in range(ITERS):
        u = log_mu[None] - lse(Z + v[:, None, :], 2)
        v = log_nu[None] - lse(Z + u[:, :, None], 1)
    return np.exp(Z + u[:, :, None] + v[:, None, :] - norm)[:, :-1, :]

@@ -1,0 +1,261 @@
+from contextlib import ExitStack
+
+import concourse.mybir as mybir
+from concourse.masks import make_identity
+
+F32 = mybir.dt.float32
+BF16 = mybir.dt.bfloat16
+U32 = mybir.dt.uint32
+U8 = mybir.dt.uint8
+FP8X4 = mybir.dt.float8_e4m3fn_x4
+ACT = mybir.ActivationFunctionType
+ALU = mybir.AluOpType
+AX = mybir.AxisListType
+
+P = 128
+PACK = 4
+K_PASS = P * PACK
+IMAGES = 4
+CHANNELS = 1536
+PIXELS = 1024
+HIDDEN = 512
+CLUSTERS = 128
+ROUNDS = 3
+PASSES = CHANNELS // K_PASS
+HID_TILES = HIDDEN // P
+HALF = 512
+HALVES = PIXELS // HALF
+BLOCKS = PIXELS // P
+BLOCKS_PER_HALF = HALF // P
+VECTOR_COLS = 256
+
+FLOPS = 2 * IMAGES * PIXELS * (HIDDEN * CHANNELS + CLUSTERS * HIDDEN)
+
+
+def regroup(copy, grouped, rows):
+    copy(
+        out=grouped.rearrange("p (c i) j -> p c j i", i=4),
+        in_=rows.rearrange("p j (c i) -> p c j i", i=4),
+    )
+
+
+def tile_salad_pa_kernel(tc, x, Ws1, bs1, Ws2, out):
+    nc = tc.nc
+    pixels_of = x.rearrange("b c h w -> b c (h w)")
+
+    with ExitStack() as ctx:
+        const = ctx.enter_context(tc.tile_pool(name="const", bufs=1))
+        raw_pool = ctx.enter_context(tc.tile_pool(name="raw", bufs=6))
+        grouped_pool = ctx.enter_context(tc.tile_pool(name="grouped", bufs=4))
+        codes_pool = ctx.enter_context(tc.tile_pool(name="codes", bufs=3))
+        hidden_pool = ctx.enter_context(tc.tile_pool(name="hidden", bufs=2))
+        image_pool = ctx.enter_context(tc.tile_pool(name="image", bufs=2))
+        small = ctx.enter_context(tc.tile_pool(name="small", bufs=4))
+        psum_acc = ctx.enter_context(tc.psum_pool(name="psum_acc", bufs=4))
+        psum_p = ctx.enter_context(tc.psum_pool(name="psum_p", bufs=2))
+        psum_vec = ctx.enter_context(tc.psum_pool(name="psum_vec", bufs=2))
+
+        def load_channels(b, g):
+            raw = raw_pool.tile([P, PACK, PIXELS], BF16)
+            rows = pixels_of[b, g * K_PASS : (g + 1) * K_PASS, :]
+            nc.sync.dma_start(out=raw[:], in_=rows.rearrange("(p j) n -> p j n", j=PACK))
+            return raw
+
+        first_raw = load_channels(0, 0)
+
+        identity = const.tile([P, P], F32)
+        make_identity(nc, identity[:])
+        mean_matrix = const.tile([P, P], F32)
+        nc.vector.memset(mean_matrix[:], 1.0 / PIXELS)
+
+        w1_raw = const.tile([P, HID_TILES * CHANNELS], BF16)
+        nc.sync.dma_start(out=w1_raw[:], in_=Ws1.rearrange("(m t) c -> m (t c)", t=HID_TILES))
+        w2_raw = const.tile([P, HIDDEN], BF16)
+        nc.scalar.dma_start(out=w2_raw[:], in_=Ws2)
+        bias_raw = const.tile([P, HID_TILES], BF16)
+        with nc.allow_non_contiguous_dma(reason="512 bias values, 4 to a partition"):
+            nc.scalar.dma_start(out=bias_raw[:], in_=bs1.rearrange("(m t) -> m t", t=HID_TILES))
+        bias = const.tile([P, HID_TILES], F32)
+        nc.vector.tensor_copy(out=bias[:], in_=bias_raw[:])
+
+        w1_planes = w1_raw[:].bitcast(F32).rearrange("m (t g p u) -> m t g u p", t=HID_TILES, g=PASSES, u=2)
+        w1_grouped = const.tile([P, PASSES, HIDDEN, 2], F32, align_bytes=64)
+        w1_codes = const.tile([P, PASSES, HIDDEN], U32, align_bytes=64)
+        w1_scales = const.tile([P, PASSES, HIDDEN], U8, align_bytes=64)
+        for g in range(PASSES):
+            for pair in range(HID_TILES // 2):
+                flipped = psum_acc.tile([P, 2, 2, P], F32, tag="acc")
+                for i in range(2):
+                    for u in range(2):
+                        nc.tensor.transpose(flipped[:, i, u, :], w1_planes[:, 2 * pair + i, g, u, :], identity[:])
+                nc.scalar.copy(
+                    out=w1_grouped[:, g, 2 * pair * P : (2 * pair + 2) * P, :].rearrange(
+                        "p (i m) u -> p i m u", i=2
+                    ),
+                    in_=flipped[:].rearrange("p i u m -> p i m u"),
+                )
+            nc.vector.quantize_mx(
+                out=w1_codes[:, g, :].bitcast(FP8X4),
+                scales=w1_scales[:, g, :],
+                in_=w1_grouped[:, g, :, :].rearrange("p m u -> p (m u)").bitcast(BF16),
+            )
+
+        w2_planes = w2_raw[:].bitcast(F32).rearrange("i (p u) -> i u p", u=2)
+        w2_grouped = const.tile([P, CLUSTERS, 2], F32, align_bytes=64)
+        w2_codes = const.tile([P, CLUSTERS], U32, align_bytes=64)
+        w2_scales = const.tile([P, CLUSTERS], U8, align_bytes=64)
+        flipped2 = psum_acc.tile([P, 2, P], F32, tag="acc")
+        for u in range(2):
+            nc.tensor.transpose(flipped2[:, u, :], w2_planes[:, u, :], identity[:])
+        nc.scalar.copy(out=w2_grouped[:], in_=flipped2[:].rearrange("p u m -> p m u"))
+        nc.vector.quantize_mx(
+            out=w2_codes[:].bitcast(FP8X4),
+            scales=w2_scales[:],
+            in_=w2_grouped[:].rearrange("p m u -> p (m u)").bitcast(BF16),
+        )
+
+        def scores_of_half(raws, h):
+            x_codes = codes_pool.tile([P, PASSES, HALF], U32, align_bytes=64)
+            x_scales = codes_pool.tile([P, PASSES, HALF], U8, align_bytes=64)
+            acc = []
+            for t in range(HID_TILES):
+                acc.append(psum_acc.tile([P, HALF], F32, tag="acc", name="acc"))
+            for g in range(PASSES):
+                rows = raws[g][:, :, h * HALF : (h + 1) * HALF]
+                x_grouped = grouped_pool.tile([P, HALF, PACK], BF16, align_bytes=64)
+                regroup(nc.vector.tensor_copy, x_grouped[:, :VECTOR_COLS, :], rows[:, :, :VECTOR_COLS])
+                regroup(nc.scalar.copy, x_grouped[:, VECTOR_COLS:, :], rows[:, :, VECTOR_COLS:])
+                nc.vector.quantize_mx(
+                    out=x_codes[:, g, :].bitcast(FP8X4),
+                    scales=x_scales[:, g, :],
+                    in_=x_grouped[:].rearrange("p n j -> p (n j)"),
+                )
+                for t in range(HID_TILES):
+                    nc.tensor.matmul_mx(
+                        out=acc[t][:],
+                        lhsT=w1_codes[:, g, t * P : (t + 1) * P].bitcast(FP8X4),
+                        lhsT_scale=w1_scales[:, g, t * P : (t + 1) * P],
+                        rhs=x_codes[:, g, :].bitcast(FP8X4),
+                        rhs_scale=x_scales[:, g, :],
+                        start=(g == 0),
+                        stop=(g == PASSES - 1),
+                    )
+            hs = hidden_pool.tile([P, HID_TILES, HALF], BF16)
+            for t in range(HID_TILES):
+                nc.scalar.activation(
+                    out=hs[:, t, :], in_=acc[t][:], func=ACT.Relu, bias=bias[:, t : t + 1], scale=1.0
+                )
+            hs_grouped = hidden_pool.tile([P, HALF, PACK], BF16, align_bytes=64)
+            regroup(nc.vector.tensor_copy, hs_grouped[:], hs[:])
+            hs_codes = hidden_pool.tile([P, HALF], U32, align_bytes=64)
+            hs_scales = hidden_pool.tile([P, HALF], U8, align_bytes=64)
+            nc.vector.quantize_mx(
+                out=hs_codes[:].bitcast(FP8X4),
+                scales=hs_scales[:],
+                in_=hs_grouped[:].rearrange("p n j -> p (n j)"),
+            )
+            p_half = psum_p.tile([P, HALF], F32, tag="p")
+            nc.tensor.matmul_mx(
+                out=p_half[:],
+                lhsT=w2_codes[:].bitcast(FP8X4),
+                lhsT_scale=w2_scales[:],
+                rhs=hs_codes[:].bitcast(FP8X4),
+                rhs_scale=hs_scales[:],
+                start=True,
+                stop=True,
+            )
+            return p_half
+
+        def sinkhorn(b, p_halves):
+            half_max = small.tile([P, HALVES], F32)
+            for h in range(HALVES):
+                nc.vector.reduce_max(out=half_max[:, h : h + 1], in_=p_halves[h][:], axis=AX.X)
+            neg_max = small.tile([P, 1], F32)
+            nc.vector.tensor_reduce(out=neg_max[:], in_=half_max[:], axis=AX.X, op=ALU.max, negate=True)
+            kern = image_pool.tile([P, PIXELS], F32)
+            half_sum = small.tile([P, HALVES], F32)
+            for h in range(HALVES):
+                nc.scalar.activation(
+                    out=kern[:, h * HALF : (h + 1) * HALF],
+                    in_=p_halves[h][:],
+                    func=ACT.Exp,
+                    bias=neg_max[:, 0:1],
+                    scale=1.0,
+                    accum_out=half_sum[:, h : h + 1],
+                )
+            kern_t = image_pool.tile([P, BLOCKS, P], F32)
+            for h in range(HALVES):
+                flipped_k = psum_p.tile([P, BLOCKS_PER_HALF, P], F32, tag="p")
+                for q in range(BLOCKS_PER_HALF):
+                    j = h * BLOCKS_PER_HALF + q
+                    nc.tensor.transpose(flipped_k[:, q, :], kern[:, j * P : (j + 1) * P], identity[:])
+                nc.scalar.copy(
+                    out=kern_t[:, h * BLOCKS_PER_HALF : (h + 1) * BLOCKS_PER_HALF, :], in_=flipped_k[:]
+                )
+
+            vec = psum_vec.tile([P, HALF], F32)
+            row_sum = small.tile([P, 1], F32)
+            nc.vector.reduce_sum(out=row_sum[:], in_=half_sum[:], axis=AX.X)
+            row_scale = small.tile([P, 2], F32)
+            nc.vector.reciprocal(out=row_scale[:, 0:1], in_=row_sum[:])
+            nc.vector.memset(row_scale[:, 1:2], 1.0)
+            for r in range(ROUNDS):
+                if r > 0:
+                    partial = small.tile([P, 1], F32)
+                    nc.vector.reduce_sum(out=partial[:], in_=col_scale[:], axis=AX.X)
+                    for j in range(BLOCKS):
+                        nc.tensor.matmul(
+                            vec[:, 8:9],
+                            lhsT=kern_t[:, j, :],
+                            rhs=col_scale[:, j : j + 1],
+                            start=(j == 0),
+                            stop=(j == BLOCKS - 1),
+                        )
+                    nc.tensor.matmul(vec[:, 9:10], lhsT=mean_matrix[:], rhs=partial[:], start=True, stop=True)
+                    row_scale = small.tile([P, 2], F32)
+                    nc.vector.reciprocal(out=row_scale[:], in_=vec[:, 8:10])
+                for j in range(BLOCKS):
+                    nc.tensor.matmul(
+                        vec[:, j : j + 1],
+                        lhsT=kern[:, j * P : (j + 1) * P],
+                        rhs=row_scale[:, 0:1],
+                        start=True,
+                        stop=True,
+                    )
+                col_sum = small.tile([P, BLOCKS], F32)
+                nc.vector.tensor_scalar(
+                    out=col_sum[:], in0=vec[:, 0:BLOCKS], scalar1=row_scale[:, 1:2], scalar2=None, op0=ALU.add
+                )
+                col_scale = small.tile([P, BLOCKS], F32)
+                nc.vector.reciprocal(out=col_scale[:], in_=col_sum[:])
+
+            result = image_pool.tile([P, PIXELS], F32)
+            for h in range(HALVES):
+                for q in range(BLOCKS_PER_HALF):
+                    j = h * BLOCKS_PER_HALF + q
+                    nc.tensor.matmul(
+                        vec[:, q * P : (q + 1) * P],
+                        lhsT=col_scale[:, j : j + 1].to_broadcast([P, P]),
+                        rhs=identity[:],
+                        start=True,
+                        stop=True,
+                    )
+                cols = slice(h * HALF, (h + 1) * HALF)
+                nc.vector.scalar_tensor_tensor(
+                    out=result[:, cols],
+                    in0=kern[:, cols],
+                    scalar=row_scale[:, 0:1],
+                    in1=vec[:],
+                    op0=ALU.mult,
+                    op1=ALU.mult,
+                )
+                nc.sync.dma_start(out=out[b, :, cols], in_=result[:, cols])
+
+        for b in range(IMAGES):
+            raws = []
+            for g in range(PASSES):
+                raws.append(first_raw if (b == 0 and g == 0) else load_channels(b, g))
+            p_halves = []
+            for h in range(HALVES):
+                p_halves.append(scores_of_half(raws, h))
+            sinkhorn(b, p_halves)

@@ -27,7 +27,11 @@ HALF = 512
 HALVES = PIXELS // HALF
 BLOCKS = PIXELS // P
 BLOCKS_PER_HALF = HALF // P
+SLICES = IMAGES * HALVES * PASSES
+UNITS = IMAGES * HALVES
+SLICES_PER_IMAGE = HALVES * PASSES
 VECTOR_COLS = 256
+LOAD_AHEAD = 6
 
 FLOPS = 2 * IMAGES * PIXELS * (HIDDEN * CHANNELS + CLUSTERS * HIDDEN)
 
@@ -45,217 +49,349 @@ def tile_salad_pa_kernel(tc, x, Ws1, bs1, Ws2, out):
 
     with ExitStack() as ctx:
         const = ctx.enter_context(tc.tile_pool(name="const", bufs=1))
-        raw_pool = ctx.enter_context(tc.tile_pool(name="raw", bufs=6))
+        raw_pool = ctx.enter_context(tc.tile_pool(name="raw", bufs=LOAD_AHEAD + 2))
         grouped_pool = ctx.enter_context(tc.tile_pool(name="grouped", bufs=4))
         codes_pool = ctx.enter_context(tc.tile_pool(name="codes", bufs=3))
         hidden_pool = ctx.enter_context(tc.tile_pool(name="hidden", bufs=2))
         image_pool = ctx.enter_context(tc.tile_pool(name="image", bufs=2))
         small = ctx.enter_context(tc.tile_pool(name="small", bufs=4))
-        psum_acc = ctx.enter_context(tc.psum_pool(name="psum_acc", bufs=4))
-        psum_p = ctx.enter_context(tc.psum_pool(name="psum_p", bufs=2))
+        psum_acc = ctx.enter_context(tc.psum_pool(name="psum_acc", bufs=HID_TILES))
+        psum_p = ctx.enter_context(tc.psum_pool(name="psum_p", bufs=HALVES))
         psum_vec = ctx.enter_context(tc.psum_pool(name="psum_vec", bufs=2))
+        ctx.enter_context(tc.manual_schedule())
 
-        def load_channels(b, g):
-            raw = raw_pool.tile([P, PACK, PIXELS], BF16)
-            rows = pixels_of[b, g * K_PASS : (g + 1) * K_PASS, :]
-            nc.sync.dma_start(out=raw[:], in_=rows.rearrange("(p j) n -> p j n", j=PACK))
-            return raw
-
-        first_raw = load_channels(0, 0)
+        raw, x_grouped, flipped_w = {}, {}, {}
+        x_codes, x_scales, acc, hs, hs_grouped, hs_codes, hs_scales, scores = {}, {}, {}, {}, {}, {}, {}, {}
+        neg_max, half_sum, kern, flipped_k, vec, row_scale, col_scale, result = {}, {}, {}, {}, {}, {}, {}, {}
+        kern_parts, kern_t_parts, row_parts, col_parts = {}, {}, {}, {}
 
         identity = const.tile([P, P], F32)
         make_identity(nc, identity[:])
-        mean_matrix = const.tile([P, P], F32)
-        nc.vector.memset(mean_matrix[:], 1.0 / PIXELS)
+        identity_bf16 = const.tile([P, P], BF16)
+        make_identity(nc, identity_bf16[:])
+        mean_of_pixels = const.tile([P, P], BF16)
+        nc.vector.memset(mean_of_pixels[:], 1.0 / PIXELS)
+        mean_of_partitions = const.tile([P, P], BF16)
+        nc.vector.memset(mean_of_partitions[:], 1.0 / P)
 
         w1_raw = const.tile([P, HID_TILES * CHANNELS], BF16)
-        nc.sync.dma_start(out=w1_raw[:], in_=Ws1.rearrange("(m t) c -> m (t c)", t=HID_TILES))
         w2_raw = const.tile([P, HIDDEN], BF16)
-        nc.scalar.dma_start(out=w2_raw[:], in_=Ws2)
         bias_raw = const.tile([P, HID_TILES], BF16)
-        with nc.allow_non_contiguous_dma(reason="512 bias values, 4 to a partition"):
-            nc.scalar.dma_start(out=bias_raw[:], in_=bs1.rearrange("(m t) -> m t", t=HID_TILES))
         bias = const.tile([P, HID_TILES], F32)
-        nc.vector.tensor_copy(out=bias[:], in_=bias_raw[:])
-
         w1_planes = w1_raw[:].bitcast(F32).rearrange("m (t g p u) -> m t g u p", t=HID_TILES, g=PASSES, u=2)
+        w2_planes = w2_raw[:].bitcast(F32).rearrange("i (p u) -> i u p", u=2)
         w1_grouped = const.tile([P, PASSES, HIDDEN, 2], F32, align_bytes=64)
         w1_codes = const.tile([P, PASSES, HIDDEN], U32, align_bytes=64)
         w1_scales = const.tile([P, PASSES, HIDDEN], U8, align_bytes=64)
-        for g in range(PASSES):
+        w2_grouped = const.tile([P, CLUSTERS, 2], F32, align_bytes=64)
+        w2_codes = const.tile([P, CLUSTERS], U32, align_bytes=64)
+        w2_scales = const.tile([P, CLUSTERS], U8, align_bytes=64)
+
+        def load_w1(g):
+            cols = slice(g * K_PASS, (g + 1) * K_PASS)
+            nc.sync.dma_start(
+                out=w1_raw[:].rearrange("m (t c) -> m t c", t=HID_TILES)[:, :, cols],
+                in_=Ws1.rearrange("(m t) c -> m t c", t=HID_TILES)[:, :, cols],
+            )
+
+        def load_small_weights():
+            nc.sync.dma_start(out=w2_raw[:], in_=Ws2)
+            with nc.allow_non_contiguous_dma(reason="512 bias values, 4 to a partition"):
+                nc.sync.dma_start(out=bias_raw[:], in_=bs1.rearrange("(m t) -> m t", t=HID_TILES))
+
+        def flip_w1(g):
             for pair in range(HID_TILES // 2):
-                flipped = psum_acc.tile([P, 2, 2, P], F32, tag="acc")
+                flipped_w[pair] = psum_p.tile([P, 2, 2, P], F32, tag="p", name="flipped_w")
                 for i in range(2):
                     for u in range(2):
-                        nc.tensor.transpose(flipped[:, i, u, :], w1_planes[:, 2 * pair + i, g, u, :], identity[:])
+                        nc.tensor.transpose(
+                            flipped_w[pair][:, i, u, :], w1_planes[:, 2 * pair + i, g, u, :], identity[:]
+                        )
+
+        def keep_w1(g):
+            for pair in range(HID_TILES // 2):
                 nc.scalar.copy(
                     out=w1_grouped[:, g, 2 * pair * P : (2 * pair + 2) * P, :].rearrange(
                         "p (i m) u -> p i m u", i=2
                     ),
-                    in_=flipped[:].rearrange("p i u m -> p i m u"),
+                    in_=flipped_w[pair][:].rearrange("p i u m -> p i m u"),
                 )
+
+        def quantise_w1(g):
             nc.vector.quantize_mx(
                 out=w1_codes[:, g, :].bitcast(FP8X4),
                 scales=w1_scales[:, g, :],
                 in_=w1_grouped[:, g, :, :].rearrange("p m u -> p (m u)").bitcast(BF16),
             )
 
-        w2_planes = w2_raw[:].bitcast(F32).rearrange("i (p u) -> i u p", u=2)
-        w2_grouped = const.tile([P, CLUSTERS, 2], F32, align_bytes=64)
-        w2_codes = const.tile([P, CLUSTERS], U32, align_bytes=64)
-        w2_scales = const.tile([P, CLUSTERS], U8, align_bytes=64)
-        flipped2 = psum_acc.tile([P, 2, P], F32, tag="acc")
-        for u in range(2):
-            nc.tensor.transpose(flipped2[:, u, :], w2_planes[:, u, :], identity[:])
-        nc.scalar.copy(out=w2_grouped[:], in_=flipped2[:].rearrange("p u m -> p m u"))
-        nc.vector.quantize_mx(
-            out=w2_codes[:].bitcast(FP8X4),
-            scales=w2_scales[:],
-            in_=w2_grouped[:].rearrange("p m u -> p (m u)").bitcast(BF16),
-        )
+        def flip_w2():
+            flipped_w[0] = psum_p.tile([P, 2, P], F32, tag="p", name="flipped_w")
+            for u in range(2):
+                nc.tensor.transpose(flipped_w[0][:, u, :], w2_planes[:, u, :], identity[:])
 
-        def scores_of_half(raws, h):
-            x_codes = codes_pool.tile([P, PASSES, HALF], U32, align_bytes=64)
-            x_scales = codes_pool.tile([P, PASSES, HALF], U8, align_bytes=64)
-            acc = []
+        def keep_w2():
+            nc.scalar.copy(out=w2_grouped[:], in_=flipped_w[0][:].rearrange("p u m -> p m u"))
+
+        def quantise_w2():
+            nc.vector.quantize_mx(
+                out=w2_codes[:].bitcast(FP8X4),
+                scales=w2_scales[:],
+                in_=w2_grouped[:].rearrange("p m u -> p (m u)").bitcast(BF16),
+            )
+
+        def widen_bias():
+            nc.vector.tensor_copy(out=bias[:], in_=bias_raw[:])
+
+        def load_x(s):
+            u, g = divmod(s, PASSES)
+            b, h = divmod(u, HALVES)
+            raw[s] = raw_pool.tile([P, PACK, HALF], BF16, name="raw")
+            rows = pixels_of[b, g * K_PASS : (g + 1) * K_PASS, h * HALF : (h + 1) * HALF]
+            nc.sync.dma_start(out=raw[s][:], in_=rows.rearrange("(p j) n -> p j n", j=PACK))
+
+        def regroup_x(s):
+            x_grouped[s] = grouped_pool.tile([P, HALF, PACK], BF16, align_bytes=64, name="x_grouped")
+            regroup(nc.vector.tensor_copy, x_grouped[s][:, :VECTOR_COLS, :], raw[s][:, :, :VECTOR_COLS])
+            regroup(nc.scalar.copy, x_grouped[s][:, VECTOR_COLS:, :], raw[s][:, :, VECTOR_COLS:])
+
+        def quantise_x(s):
+            u, g = divmod(s, PASSES)
+            if g == 0:
+                x_codes[u] = codes_pool.tile([P, PASSES, HALF], U32, align_bytes=64, name="x_codes")
+                x_scales[u] = codes_pool.tile([P, PASSES, HALF], U8, align_bytes=64, name="x_scales")
+            nc.vector.quantize_mx(
+                out=x_codes[u][:, g, :].bitcast(FP8X4),
+                scales=x_scales[u][:, g, :],
+                in_=x_grouped[s][:].rearrange("p n j -> p (n j)"),
+            )
+
+        def first_product(s):
+            u, g = divmod(s, PASSES)
             for t in range(HID_TILES):
-                acc.append(psum_acc.tile([P, HALF], F32, tag="acc", name="acc"))
-            for g in range(PASSES):
-                rows = raws[g][:, :, h * HALF : (h + 1) * HALF]
-                x_grouped = grouped_pool.tile([P, HALF, PACK], BF16, align_bytes=64)
-                regroup(nc.vector.tensor_copy, x_grouped[:, :VECTOR_COLS, :], rows[:, :, :VECTOR_COLS])
-                regroup(nc.scalar.copy, x_grouped[:, VECTOR_COLS:, :], rows[:, :, VECTOR_COLS:])
-                nc.vector.quantize_mx(
-                    out=x_codes[:, g, :].bitcast(FP8X4),
-                    scales=x_scales[:, g, :],
-                    in_=x_grouped[:].rearrange("p n j -> p (n j)"),
+                if g == 0:
+                    acc[u, t] = psum_acc.tile([P, HALF], F32, name="acc")
+                nc.tensor.matmul_mx(
+                    out=acc[u, t][:],
+                    lhsT=w1_codes[:, g, t * P : (t + 1) * P].bitcast(FP8X4),
+                    lhsT_scale=w1_scales[:, g, t * P : (t + 1) * P],
+                    rhs=x_codes[u][:, g, :].bitcast(FP8X4),
+                    rhs_scale=x_scales[u][:, g, :],
+                    start=(g == 0),
+                    stop=(g == PASSES - 1),
                 )
-                for t in range(HID_TILES):
-                    nc.tensor.matmul_mx(
-                        out=acc[t][:],
-                        lhsT=w1_codes[:, g, t * P : (t + 1) * P].bitcast(FP8X4),
-                        lhsT_scale=w1_scales[:, g, t * P : (t + 1) * P],
-                        rhs=x_codes[:, g, :].bitcast(FP8X4),
-                        rhs_scale=x_scales[:, g, :],
-                        start=(g == 0),
-                        stop=(g == PASSES - 1),
-                    )
-            hs = hidden_pool.tile([P, HID_TILES, HALF], BF16)
+
+        def bias_relu(u):
+            hs[u] = hidden_pool.tile([P, HID_TILES, HALF], BF16, name="hs")
             for t in range(HID_TILES):
                 nc.scalar.activation(
-                    out=hs[:, t, :], in_=acc[t][:], func=ACT.Relu, bias=bias[:, t : t + 1], scale=1.0
+                    out=hs[u][:, t, :], in_=acc[u, t][:], func=ACT.Relu, bias=bias[:, t : t + 1], scale=1.0
                 )
-            hs_grouped = hidden_pool.tile([P, HALF, PACK], BF16, align_bytes=64)
-            regroup(nc.vector.tensor_copy, hs_grouped[:], hs[:])
-            hs_codes = hidden_pool.tile([P, HALF], U32, align_bytes=64)
-            hs_scales = hidden_pool.tile([P, HALF], U8, align_bytes=64)
+
+        def regroup_hs(u):
+            hs_grouped[u] = hidden_pool.tile([P, HALF, PACK], BF16, align_bytes=64, name="hs_grouped")
+            regroup(nc.vector.tensor_copy, hs_grouped[u][:], hs[u][:])
+
+        def quantise_hs(u):
+            hs_codes[u] = hidden_pool.tile([P, HALF], U32, align_bytes=64, name="hs_codes")
+            hs_scales[u] = hidden_pool.tile([P, HALF], U8, align_bytes=64, name="hs_scales")
             nc.vector.quantize_mx(
-                out=hs_codes[:].bitcast(FP8X4),
-                scales=hs_scales[:],
-                in_=hs_grouped[:].rearrange("p n j -> p (n j)"),
+                out=hs_codes[u][:].bitcast(FP8X4),
+                scales=hs_scales[u][:],
+                in_=hs_grouped[u][:].rearrange("p n j -> p (n j)"),
             )
-            p_half = psum_p.tile([P, HALF], F32, tag="p")
+
+        def second_product(u):
+            scores[u] = psum_p.tile([P, HALF], F32, tag="p", name="scores")
             nc.tensor.matmul_mx(
-                out=p_half[:],
+                out=scores[u][:],
                 lhsT=w2_codes[:].bitcast(FP8X4),
                 lhsT_scale=w2_scales[:],
-                rhs=hs_codes[:].bitcast(FP8X4),
-                rhs_scale=hs_scales[:],
+                rhs=hs_codes[u][:].bitcast(FP8X4),
+                rhs_scale=hs_scales[u][:],
                 start=True,
                 stop=True,
             )
-            return p_half
 
-        def sinkhorn(b, p_halves):
+        def row_maximum(b):
             half_max = small.tile([P, HALVES], F32)
             for h in range(HALVES):
-                nc.vector.reduce_max(out=half_max[:, h : h + 1], in_=p_halves[h][:], axis=AX.X)
-            neg_max = small.tile([P, 1], F32)
-            nc.vector.tensor_reduce(out=neg_max[:], in_=half_max[:], axis=AX.X, op=ALU.max, negate=True)
-            kern = image_pool.tile([P, PIXELS], F32)
-            half_sum = small.tile([P, HALVES], F32)
+                nc.vector.reduce_max(out=half_max[:, h : h + 1], in_=scores[HALVES * b + h][:], axis=AX.X)
+            neg_max[b] = small.tile([P, 1], F32, name="neg_max")
+            nc.vector.tensor_reduce(out=neg_max[b][:], in_=half_max[:], axis=AX.X, op=ALU.max, negate=True)
+
+        def kernel_matrix(b):
+            kern[b] = image_pool.tile([P, PIXELS], F32, name="kern")
+            half_sum[b] = small.tile([P, HALVES], F32, name="half_sum")
             for h in range(HALVES):
                 nc.scalar.activation(
-                    out=kern[:, h * HALF : (h + 1) * HALF],
-                    in_=p_halves[h][:],
+                    out=kern[b][:, h * HALF : (h + 1) * HALF],
+                    in_=scores[HALVES * b + h][:],
                     func=ACT.Exp,
-                    bias=neg_max[:, 0:1],
+                    bias=neg_max[b][:, 0:1],
                     scale=1.0,
-                    accum_out=half_sum[:, h : h + 1],
-                )
-            kern_t = image_pool.tile([P, BLOCKS, P], F32)
-            for h in range(HALVES):
-                flipped_k = psum_p.tile([P, BLOCKS_PER_HALF, P], F32, tag="p")
-                for q in range(BLOCKS_PER_HALF):
-                    j = h * BLOCKS_PER_HALF + q
-                    nc.tensor.transpose(flipped_k[:, q, :], kern[:, j * P : (j + 1) * P], identity[:])
-                nc.scalar.copy(
-                    out=kern_t[:, h * BLOCKS_PER_HALF : (h + 1) * BLOCKS_PER_HALF, :], in_=flipped_k[:]
+                    accum_out=half_sum[b][:, h : h + 1],
                 )
 
-            vec = psum_vec.tile([P, HALF], F32)
-            row_sum = small.tile([P, 1], F32)
-            nc.vector.reduce_sum(out=row_sum[:], in_=half_sum[:], axis=AX.X)
-            row_scale = small.tile([P, 2], F32)
-            nc.vector.reciprocal(out=row_scale[:, 0:1], in_=row_sum[:])
-            nc.vector.memset(row_scale[:, 1:2], 1.0)
-            for r in range(ROUNDS):
-                if r > 0:
-                    partial = small.tile([P, 1], F32)
-                    nc.vector.reduce_sum(out=partial[:], in_=col_scale[:], axis=AX.X)
-                    for j in range(BLOCKS):
-                        nc.tensor.matmul(
-                            vec[:, 8:9],
-                            lhsT=kern_t[:, j, :],
-                            rhs=col_scale[:, j : j + 1],
-                            start=(j == 0),
-                            stop=(j == BLOCKS - 1),
-                        )
-                    nc.tensor.matmul(vec[:, 9:10], lhsT=mean_matrix[:], rhs=partial[:], start=True, stop=True)
-                    row_scale = small.tile([P, 2], F32)
-                    nc.vector.reciprocal(out=row_scale[:], in_=vec[:, 8:10])
-                for j in range(BLOCKS):
+        def split(parts, values):
+            nc.vector.tensor_copy(out=parts[:, :, 0], in_=values)
+            nc.vector.tensor_tensor(out=parts[:, :, 1], in0=values, in1=parts[:, :, 0], op=ALU.subtract)
+
+        def split_kernel(b):
+            for part in range(2):
+                kern_parts[b, part] = image_pool.tile([P, PIXELS], BF16, name="kern_part%d" % part)
+            nc.vector.tensor_copy(out=kern_parts[b, 0][:], in_=kern[b][:])
+            nc.vector.tensor_tensor(out=kern_parts[b, 1][:], in0=kern[b][:], in1=kern_parts[b, 0][:], op=ALU.subtract)
+
+        def invert_row_sums(b, row_sum):
+            row_scale[b] = small.tile([P, 2], F32, name="row_scale")
+            nc.vector.reciprocal(out=row_scale[b][:], in_=row_sum[:])
+            row_parts[b] = small.tile([P, 2, 2], BF16, name="row_parts")
+            split(row_parts[b], row_scale[b][:])
+
+        def first_row_scale(b):
+            row_sum = small.tile([P, 2], F32)
+            nc.vector.reduce_sum(out=row_sum[:, 0:1], in_=half_sum[b][:], axis=AX.X)
+            nc.vector.memset(row_sum[:, 1:2], 1.0)
+            invert_row_sums(b, row_sum)
+            vec[b] = psum_vec.tile([P, HALF], F32, name="vec")
+
+        def flip_kernel(b, part):
+            flipped_k[b] = psum_p.tile([P, BLOCKS, P], BF16, tag="p", name="flipped_k")
+            for j in range(BLOCKS):
+                nc.tensor.transpose(flipped_k[b][:, j, :], kern_parts[b, part][:, j * P : (j + 1) * P], identity_bf16[:])
+
+        def keep_flipped(b, part):
+            kern_t_parts[b, part] = image_pool.tile([P, BLOCKS, P], BF16, name="kern_t_part%d" % part)
+            nc.scalar.copy(out=kern_t_parts[b, part][:], in_=flipped_k[b][:])
+
+        def column_sums(b):
+            sums = vec[b][:, 0 : 2 * BLOCKS].rearrange("p (j q) -> p j q", q=2)
+            nc.tensor.matmul(
+                sums,
+                lhsT=mean_of_partitions[:],
+                rhs=row_parts[b][:, 1:2, :].to_broadcast([P, BLOCKS, 2]),
+                start=True,
+                stop=False,
+            )
+            for j in range(BLOCKS):
+                for part in range(2):
                     nc.tensor.matmul(
-                        vec[:, j : j + 1],
-                        lhsT=kern[:, j * P : (j + 1) * P],
-                        rhs=row_scale[:, 0:1],
-                        start=True,
-                        stop=True,
+                        sums[:, j, :],
+                        lhsT=kern_parts[b, part][:, j * P : (j + 1) * P],
+                        rhs=row_parts[b][:, 0, :],
+                        start=False,
+                        stop=(j == BLOCKS - 1 and part == 1),
                     )
-                col_sum = small.tile([P, BLOCKS], F32)
-                nc.vector.tensor_scalar(
-                    out=col_sum[:], in0=vec[:, 0:BLOCKS], scalar1=row_scale[:, 1:2], scalar2=None, op0=ALU.add
-                )
-                col_scale = small.tile([P, BLOCKS], F32)
-                nc.vector.reciprocal(out=col_scale[:], in_=col_sum[:])
 
-            result = image_pool.tile([P, PIXELS], F32)
-            for h in range(HALVES):
-                for q in range(BLOCKS_PER_HALF):
-                    j = h * BLOCKS_PER_HALF + q
+        def column_scale(b):
+            col_sum = small.tile([P, BLOCKS], F32)
+            nc.vector.reduce_sum(
+                out=col_sum[:], in_=vec[b][:, 0 : 2 * BLOCKS].rearrange("p (j q) -> p j q", q=2), axis=AX.X
+            )
+            col_scale[b] = small.tile([P, BLOCKS], F32, name="col_scale")
+            nc.vector.reciprocal(out=col_scale[b][:], in_=col_sum[:])
+
+        def row_sums(b):
+            col_parts[b] = small.tile([P, BLOCKS, 2], BF16, name="col_parts")
+            split(col_parts[b], col_scale[b][:])
+            sums = vec[b][:, 2 * BLOCKS : 6 * BLOCKS].rearrange("p (s j q) -> p s j q", s=2, q=2)
+            for j in range(BLOCKS):
+                for part in range(2):
                     nc.tensor.matmul(
-                        vec[:, q * P : (q + 1) * P],
-                        lhsT=col_scale[:, j : j + 1].to_broadcast([P, P]),
-                        rhs=identity[:],
-                        start=True,
-                        stop=True,
+                        sums[:, 0, j, :],
+                        lhsT=kern_t_parts[b, part][:, j, :],
+                        rhs=col_parts[b][:, j, :],
+                        start=(part == 0),
+                        stop=(part == 1),
                     )
-                cols = slice(h * HALF, (h + 1) * HALF)
-                nc.vector.scalar_tensor_tensor(
-                    out=result[:, cols],
-                    in0=kern[:, cols],
-                    scalar=row_scale[:, 0:1],
-                    in1=vec[:],
-                    op0=ALU.mult,
-                    op1=ALU.mult,
-                )
-                nc.sync.dma_start(out=out[b, :, cols], in_=result[:, cols])
+            nc.tensor.matmul(sums[:, 1, :, :], lhsT=mean_of_pixels[:], rhs=col_parts[b][:], start=True, stop=True)
 
-        for b in range(IMAGES):
-            raws = []
-            for g in range(PASSES):
-                raws.append(first_raw if (b == 0 and g == 0) else load_channels(b, g))
-            p_halves = []
-            for h in range(HALVES):
-                p_halves.append(scores_of_half(raws, h))
-            sinkhorn(b, p_halves)
+        def next_row_scale(b):
+            row_sum = small.tile([P, 2], F32)
+            nc.vector.reduce_sum(
+                out=row_sum[:], in_=vec[b][:, 2 * BLOCKS : 6 * BLOCKS].rearrange("p (s c) -> p s c", s=2), axis=AX.X
+            )
+            invert_row_sums(b, row_sum)
+
+        def spread(b, h):
+            for q in range(BLOCKS_PER_HALF):
+                j = h * BLOCKS_PER_HALF + q
+                nc.tensor.transpose(
+                    vec[b][:, q * P : (q + 1) * P], col_scale[b][:, j : j + 1].to_broadcast([P, P]), identity[:]
+                )
+
+        def finish(b, h):
+            if h == 0:
+                result[b] = image_pool.tile([P, PIXELS], F32, name="result")
+            cols = slice(h * HALF, (h + 1) * HALF)
+            nc.vector.scalar_tensor_tensor(
+                out=result[b][:, cols],
+                in0=kern[b][:, cols],
+                scalar=row_scale[b][:, 0:1],
+                in1=vec[b][:],
+                op0=ALU.mult,
+                op1=ALU.mult,
+            )
+            nc.sync.dma_start(out=out[b, :, cols], in_=result[b][:, cols])
+
+        sinkhorn_steps = [
+            lambda b: row_maximum(b),
+            lambda b: kernel_matrix(b),
+            lambda b: (first_row_scale(b), split_kernel(b), flip_kernel(b, 0), column_sums(b)),
+            lambda b: (keep_flipped(b, 0), flip_kernel(b, 1), column_scale(b)),
+            lambda b: (keep_flipped(b, 1), row_sums(b)),
+            lambda b: (next_row_scale(b), column_sums(b)),
+            lambda b: (column_scale(b), row_sums(b)),
+            lambda b: (next_row_scale(b), column_sums(b)),
+            lambda b: (column_scale(b), spread(b, 0)),
+            lambda b: (finish(b, 0), spread(b, 1)),
+            lambda b: finish(b, 1),
+        ]
+
+        def unit_ending_at(s):
+            u, g = divmod(s, PASSES)
+            return u if (g == PASSES - 1 and 0 <= u < UNITS) else None
+
+        first_step = SLICES_PER_IMAGE - 1 + 6
+        ticks = (IMAGES - 1) * SLICES_PER_IMAGE + first_step + len(sinkhorn_steps)
+
+        for g in range(PASSES):
+            load_x(g)
+            load_w1(g)
+        load_small_weights()
+        for s in range(PASSES, LOAD_AHEAD):
+            load_x(s)
+
+        for t in range(ticks):
+            if t + LOAD_AHEAD < SLICES:
+                load_x(t + LOAD_AHEAD)
+            if 2 <= t < PASSES + 2:
+                quantise_w1(t - 2)
+            if t == PASSES + 1:
+                widen_bias()
+            if t == PASSES + 2:
+                quantise_w2()
+            if unit_ending_at(t - 3) is not None:
+                bias_relu(unit_ending_at(t - 3))
+            if 0 <= t - 2 < SLICES:
+                quantise_x(t - 2)
+                first_product(t - 2)
+            if unit_ending_at(t - 5) is not None:
+                quantise_hs(unit_ending_at(t - 5))
+                second_product(unit_ending_at(t - 5))
+            if t < SLICES:
+                regroup_x(t)
+            if unit_ending_at(t - 4) is not None:
+                regroup_hs(unit_ending_at(t - 4))
+            if 1 <= t < PASSES + 1:
+                keep_w1(t - 1)
+            if t == PASSES + 1:
+                keep_w2()
+            if t < PASSES:
+                flip_w1(t)
+            if t == PASSES:
+                flip_w2()
+            for k in range(len(sinkhorn_steps)):
+                b, rest = divmod(t - first_step - k, SLICES_PER_IMAGE)
+                if rest == 0 and 0 <= b < IMAGES:
+                    sinkhorn_steps[k](b)

@@ -30,7 +30,7 @@ BLOCKS_PER_HALF = HALF // P
 SLICES = IMAGES * HALVES * PASSES
 UNITS = IMAGES * HALVES
 SLICES_PER_IMAGE = HALVES * PASSES
-VECTOR_COLS = 256
+VECTOR_COLS = 192
 LOAD_AHEAD = 6
 
 FLOPS = 2 * IMAGES * PIXELS * (HIDDEN * CHANNELS + CLUSTERS * HIDDEN)
@@ -58,7 +58,6 @@ def tile_salad_pa_kernel(tc, x, Ws1, bs1, Ws2, out):
         psum_acc = ctx.enter_context(tc.psum_pool(name="psum_acc", bufs=HID_TILES))
         psum_p = ctx.enter_context(tc.psum_pool(name="psum_p", bufs=HALVES))
         psum_vec = ctx.enter_context(tc.psum_pool(name="psum_vec", bufs=2))
-        ctx.enter_context(tc.manual_schedule())
 
         raw, x_grouped, flipped_w = {}, {}, {}
         x_codes, x_scales, acc, hs, hs_grouped, hs_codes, hs_scales, scores = {}, {}, {}, {}, {}, {}, {}, {}

@@ -30,7 +30,7 @@ BLOCKS_PER_HALF = HALF // P
 SLICES = IMAGES * HALVES * PASSES
 UNITS = IMAGES * HALVES
 SLICES_PER_IMAGE = HALVES * PASSES
-VECTOR_COLS = 192
+VECTOR_COLS = 256
 LOAD_AHEAD = 6
 
 FLOPS = 2 * IMAGES * PIXELS * (HIDDEN * CHANNELS + CLUSTERS * HIDDEN)
@@ -53,7 +53,7 @@ def tile_salad_pa_kernel(tc, x, Ws1, bs1, Ws2, out):
         grouped_pool = ctx.enter_context(tc.tile_pool(name="grouped", bufs=4))
         codes_pool = ctx.enter_context(tc.tile_pool(name="codes", bufs=3))
         hidden_pool = ctx.enter_context(tc.tile_pool(name="hidden", bufs=2))
-        image_pool = ctx.enter_context(tc.tile_pool(name="image", bufs=2))
+        image_pool = ctx.enter_context(tc.tile_pool(name="image", bufs=3))
         small = ctx.enter_context(tc.tile_pool(name="small", bufs=4))
         psum_acc = ctx.enter_context(tc.psum_pool(name="psum_acc", bufs=HID_TILES))
         psum_p = ctx.enter_context(tc.psum_pool(name="psum_p", bufs=HALVES))
@@ -333,26 +333,38 @@ def tile_salad_pa_kernel(tc, x, Ws1, bs1, Ws2, out):
             )
             nc.sync.dma_start(out=out[b, :, cols], in_=result[b][:, cols])
 
-        sinkhorn_steps = [
-            lambda b: row_maximum(b),
-            lambda b: kernel_matrix(b),
-            lambda b: (first_row_scale(b), split_kernel(b), flip_kernel(b, 0), column_sums(b)),
-            lambda b: (keep_flipped(b, 0), flip_kernel(b, 1), column_scale(b)),
-            lambda b: (keep_flipped(b, 1), row_sums(b)),
-            lambda b: (next_row_scale(b), column_sums(b)),
-            lambda b: (column_scale(b), row_sums(b)),
-            lambda b: (next_row_scale(b), column_sums(b)),
-            lambda b: (column_scale(b), spread(b, 0)),
-            lambda b: (finish(b, 0), spread(b, 1)),
-            lambda b: finish(b, 1),
-        ]
+        def sinkhorn_start(b):
+            row_maximum(b)
+            kernel_matrix(b)
+            split_kernel(b)
+            for part in range(2):
+                flip_kernel(b, part)
+                keep_flipped(b, part)
 
-        def unit_ending_at(s):
-            u, g = divmod(s, PASSES)
-            return u if (g == PASSES - 1 and 0 <= u < UNITS) else None
+        def sinkhorn_rounds(b):
+            first_row_scale(b)
+            for r in range(ROUNDS):
+                if r > 0:
+                    row_sums(b)
+                    next_row_scale(b)
+                column_sums(b)
+                column_scale(b)
+            for h in range(HALVES):
+                spread(b, h)
+                finish(b, h)
 
-        first_step = SLICES_PER_IMAGE - 1 + 6
-        ticks = (IMAGES - 1) * SLICES_PER_IMAGE + first_step + len(sinkhorn_steps)
+        def scores_of_half(u):
+            for g in range(PASSES):
+                s = u * PASSES + g
+                if s + LOAD_AHEAD < SLICES:
+                    load_x(s + LOAD_AHEAD)
+                regroup_x(s)
+                quantise_x(s)
+                first_product(s)
+            bias_relu(u)
+            regroup_hs(u)
+            quantise_hs(u)
+            second_product(u)
 
         for g in range(PASSES):
             load_x(g)
@@ -360,37 +372,19 @@ def tile_salad_pa_kernel(tc, x, Ws1, bs1, Ws2, out):
         load_small_weights()
         for s in range(PASSES, LOAD_AHEAD):
             load_x(s)
+        for g in range(PASSES):
+            flip_w1(g)
+            keep_w1(g)
+            quantise_w1(g)
+        flip_w2()
+        keep_w2()
+        quantise_w2()
+        widen_bias()
 
-        for t in range(ticks):
-            if t + LOAD_AHEAD < SLICES:
-                load_x(t + LOAD_AHEAD)
-            if 2 <= t < PASSES + 2:
-                quantise_w1(t - 2)
-            if t == PASSES + 1:
-                widen_bias()
-            if t == PASSES + 2:
-                quantise_w2()
-            if unit_ending_at(t - 3) is not None:
-                bias_relu(unit_ending_at(t - 3))
-            if 0 <= t - 2 < SLICES:
-                quantise_x(t - 2)
-                first_product(t - 2)
-            if unit_ending_at(t - 5) is not None:
-                quantise_hs(unit_ending_at(t - 5))
-                second_product(unit_ending_at(t - 5))
-            if t < SLICES:
-                regroup_x(t)
-            if unit_ending_at(t - 4) is not None:
-                regroup_hs(unit_ending_at(t - 4))
-            if 1 <= t < PASSES + 1:
-                keep_w1(t - 1)
-            if t == PASSES + 1:
-                keep_w2()
-            if t < PASSES:
-                flip_w1(t)
-            if t == PASSES:
-                flip_w2()
-            for k in range(len(sinkhorn_steps)):
-                b, rest = divmod(t - first_step - k, SLICES_PER_IMAGE)
-                if rest == 0 and 0 <= b < IMAGES:
-                    sinkhorn_steps[k](b)
+        for b in range(IMAGES):
+            scores_of_half(b * HALVES)
+            if b > 0:
+                sinkhorn_rounds(b - 1)
+            scores_of_half(b * HALVES + 1)
+            sinkhorn_start(b)
+        sinkhorn_rounds(IMAGES - 1)

@@ -27,10 +27,9 @@ HALF = 512
 HALVES = PIXELS // HALF
 BLOCKS = PIXELS // P
 BLOCKS_PER_HALF = HALF // P
+PARTS = 2
 SLICES = IMAGES * HALVES * PASSES
-UNITS = IMAGES * HALVES
-SLICES_PER_IMAGE = HALVES * PASSES
-VECTOR_COLS = 256
+VECTOR_COLS = 288
 LOAD_AHEAD = 6
 
 FLOPS = 2 * IMAGES * PIXELS * (HIDDEN * CHANNELS + CLUSTERS * HIDDEN)
@@ -38,14 +37,14 @@ FLOPS = 2 * IMAGES * PIXELS * (HIDDEN * CHANNELS + CLUSTERS * HIDDEN)
 
 def regroup(copy, grouped, rows):
     copy(
-        out=grouped.rearrange("p (c i) j -> p c j i", i=4),
-        in_=rows.rearrange("p j (c i) -> p c j i", i=4),
+        out=grouped.rearrange("p (run n) j -> p run j n", n=4),
+        in_=rows.rearrange("p j (run n) -> p run j n", n=4),
     )
 
 
 def tile_salad_pa_kernel(tc, x, Ws1, bs1, Ws2, out):
     nc = tc.nc
-    pixels_of = x.rearrange("b c h w -> b c (h w)")
+    pixels_of = x.rearrange("img c row col -> img c (row col)")
 
     with ExitStack() as ctx:
         const = ctx.enter_context(tc.tile_pool(name="const", bufs=1))
@@ -56,13 +55,8 @@ def tile_salad_pa_kernel(tc, x, Ws1, bs1, Ws2, out):
         image_pool = ctx.enter_context(tc.tile_pool(name="image", bufs=3))
         small = ctx.enter_context(tc.tile_pool(name="small", bufs=4))
         psum_acc = ctx.enter_context(tc.psum_pool(name="psum_acc", bufs=HID_TILES))
-        psum_p = ctx.enter_context(tc.psum_pool(name="psum_p", bufs=HALVES))
+        psum_scores = ctx.enter_context(tc.psum_pool(name="psum_scores", bufs=HALVES))
         psum_vec = ctx.enter_context(tc.psum_pool(name="psum_vec", bufs=2))
-
-        raw, x_grouped, flipped_w = {}, {}, {}
-        x_codes, x_scales, acc, hs, hs_grouped, hs_codes, hs_scales, scores = {}, {}, {}, {}, {}, {}, {}, {}
-        neg_max, half_sum, kern, flipped_k, vec, row_scale, col_scale, result = {}, {}, {}, {}, {}, {}, {}, {}
-        kern_parts, kern_t_parts, row_parts, col_parts = {}, {}, {}, {}
 
         identity = const.tile([P, P], F32)
         make_identity(nc, identity[:])
@@ -77,8 +71,8 @@ def tile_salad_pa_kernel(tc, x, Ws1, bs1, Ws2, out):
         w2_raw = const.tile([P, HIDDEN], BF16)
         bias_raw = const.tile([P, HID_TILES], BF16)
         bias = const.tile([P, HID_TILES], F32)
-        w1_planes = w1_raw[:].bitcast(F32).rearrange("m (t g p u) -> m t g u p", t=HID_TILES, g=PASSES, u=2)
-        w2_planes = w2_raw[:].bitcast(F32).rearrange("i (p u) -> i u p", u=2)
+        w1_words = w1_raw[:].bitcast(F32).rearrange("m (t g p w) -> m t g w p", t=HID_TILES, g=PASSES, w=2)
+        w2_words = w2_raw[:].bitcast(F32).rearrange("m (p w) -> m w p", w=2)
         w1_grouped = const.tile([P, PASSES, HIDDEN, 2], F32, align_bytes=64)
         w1_codes = const.tile([P, PASSES, HIDDEN], U32, align_bytes=64)
         w1_scales = const.tile([P, PASSES, HIDDEN], U8, align_bytes=64)
@@ -98,273 +92,209 @@ def tile_salad_pa_kernel(tc, x, Ws1, bs1, Ws2, out):
             with nc.allow_non_contiguous_dma(reason="512 bias values, 4 to a partition"):
                 nc.sync.dma_start(out=bias_raw[:], in_=bs1.rearrange("(m t) -> m t", t=HID_TILES))
 
-        def flip_w1(g):
+        def prepare_w1(g):
+            flipped = []
             for pair in range(HID_TILES // 2):
-                flipped_w[pair] = psum_p.tile([P, 2, 2, P], F32, tag="p", name="flipped_w")
-                for i in range(2):
-                    for u in range(2):
+                flipped.append(psum_scores.tile([P, 2, 2, P], F32, tag="scores", name="flipped_w"))
+                for member in range(2):
+                    for w in range(2):
                         nc.tensor.transpose(
-                            flipped_w[pair][:, i, u, :], w1_planes[:, 2 * pair + i, g, u, :], identity[:]
+                            flipped[pair][:, member, w, :], w1_words[:, 2 * pair + member, g, w, :], identity[:]
                         )
-
-        def keep_w1(g):
             for pair in range(HID_TILES // 2):
                 nc.scalar.copy(
                     out=w1_grouped[:, g, 2 * pair * P : (2 * pair + 2) * P, :].rearrange(
-                        "p (i m) u -> p i m u", i=2
+                        "p (member m) w -> p member m w", member=2
                     ),
-                    in_=flipped_w[pair][:].rearrange("p i u m -> p i m u"),
+                    in_=flipped[pair][:].rearrange("p member w m -> p member m w"),
                 )
-
-        def quantise_w1(g):
             nc.vector.quantize_mx(
                 out=w1_codes[:, g, :].bitcast(FP8X4),
                 scales=w1_scales[:, g, :],
-                in_=w1_grouped[:, g, :, :].rearrange("p m u -> p (m u)").bitcast(BF16),
+                in_=w1_grouped[:, g, :, :].rearrange("p m w -> p (m w)").bitcast(BF16),
             )
 
-        def flip_w2():
-            flipped_w[0] = psum_p.tile([P, 2, P], F32, tag="p", name="flipped_w")
-            for u in range(2):
-                nc.tensor.transpose(flipped_w[0][:, u, :], w2_planes[:, u, :], identity[:])
-
-        def keep_w2():
-            nc.scalar.copy(out=w2_grouped[:], in_=flipped_w[0][:].rearrange("p u m -> p m u"))
-
-        def quantise_w2():
+        def prepare_small_weights():
+            flipped = psum_scores.tile([P, 2, P], F32, tag="scores", name="flipped_w")
+            for w in range(2):
+                nc.tensor.transpose(flipped[:, w, :], w2_words[:, w, :], identity[:])
+            nc.scalar.copy(out=w2_grouped[:], in_=flipped[:].rearrange("p w m -> p m w"))
             nc.vector.quantize_mx(
                 out=w2_codes[:].bitcast(FP8X4),
                 scales=w2_scales[:],
-                in_=w2_grouped[:].rearrange("p m u -> p (m u)").bitcast(BF16),
+                in_=w2_grouped[:].rearrange("p m w -> p (m w)").bitcast(BF16),
             )
-
-        def widen_bias():
             nc.vector.tensor_copy(out=bias[:], in_=bias_raw[:])
 
+        raw = {}
+
         def load_x(s):
-            u, g = divmod(s, PASSES)
-            b, h = divmod(u, HALVES)
+            img, rest = divmod(s, HALVES * PASSES)
+            h, g = divmod(rest, PASSES)
             raw[s] = raw_pool.tile([P, PACK, HALF], BF16, name="raw")
-            rows = pixels_of[b, g * K_PASS : (g + 1) * K_PASS, h * HALF : (h + 1) * HALF]
+            rows = pixels_of[img, g * K_PASS : (g + 1) * K_PASS, h * HALF : (h + 1) * HALF]
             nc.sync.dma_start(out=raw[s][:], in_=rows.rearrange("(p j) n -> p j n", j=PACK))
 
-        def regroup_x(s):
-            x_grouped[s] = grouped_pool.tile([P, HALF, PACK], BF16, align_bytes=64, name="x_grouped")
-            regroup(nc.vector.tensor_copy, x_grouped[s][:, :VECTOR_COLS, :], raw[s][:, :, :VECTOR_COLS])
-            regroup(nc.scalar.copy, x_grouped[s][:, VECTOR_COLS:, :], raw[s][:, :, VECTOR_COLS:])
-
-        def quantise_x(s):
-            u, g = divmod(s, PASSES)
-            if g == 0:
-                x_codes[u] = codes_pool.tile([P, PASSES, HALF], U32, align_bytes=64, name="x_codes")
-                x_scales[u] = codes_pool.tile([P, PASSES, HALF], U8, align_bytes=64, name="x_scales")
-            nc.vector.quantize_mx(
-                out=x_codes[u][:, g, :].bitcast(FP8X4),
-                scales=x_scales[u][:, g, :],
-                in_=x_grouped[s][:].rearrange("p n j -> p (n j)"),
-            )
-
-        def first_product(s):
-            u, g = divmod(s, PASSES)
-            for t in range(HID_TILES):
-                if g == 0:
-                    acc[u, t] = psum_acc.tile([P, HALF], F32, name="acc")
-                nc.tensor.matmul_mx(
-                    out=acc[u, t][:],
-                    lhsT=w1_codes[:, g, t * P : (t + 1) * P].bitcast(FP8X4),
-                    lhsT_scale=w1_scales[:, g, t * P : (t + 1) * P],
-                    rhs=x_codes[u][:, g, :].bitcast(FP8X4),
-                    rhs_scale=x_scales[u][:, g, :],
-                    start=(g == 0),
-                    stop=(g == PASSES - 1),
+        def scores_of_half(img, h):
+            x_codes = codes_pool.tile([P, PASSES, HALF], U32, align_bytes=64)
+            x_scales = codes_pool.tile([P, PASSES, HALF], U8, align_bytes=64)
+            acc = []
+            for g in range(PASSES):
+                s = (img * HALVES + h) * PASSES + g
+                if s + LOAD_AHEAD < SLICES:
+                    load_x(s + LOAD_AHEAD)
+                x_grouped = grouped_pool.tile([P, HALF, PACK], BF16, align_bytes=64)
+                regroup(nc.vector.tensor_copy, x_grouped[:, :VECTOR_COLS, :], raw[s][:, :, :VECTOR_COLS])
+                regroup(nc.scalar.copy, x_grouped[:, VECTOR_COLS:, :], raw[s][:, :, VECTOR_COLS:])
+                nc.vector.quantize_mx(
+                    out=x_codes[:, g, :].bitcast(FP8X4),
+                    scales=x_scales[:, g, :],
+                    in_=x_grouped[:].rearrange("p n j -> p (n j)"),
                 )
-
-        def bias_relu(u):
-            hs[u] = hidden_pool.tile([P, HID_TILES, HALF], BF16, name="hs")
+                for t in range(HID_TILES):
+                    if g == 0:
+                        acc.append(psum_acc.tile([P, HALF], F32, name="acc"))
+                    nc.tensor.matmul_mx(
+                        out=acc[t][:],
+                        lhsT=w1_codes[:, g, t * P : (t + 1) * P].bitcast(FP8X4),
+                        lhsT_scale=w1_scales[:, g, t * P : (t + 1) * P],
+                        rhs=x_codes[:, g, :].bitcast(FP8X4),
+                        rhs_scale=x_scales[:, g, :],
+                        start=(g == 0),
+                        stop=(g == PASSES - 1),
+                    )
+            hs = hidden_pool.tile([P, HID_TILES, HALF], BF16)
             for t in range(HID_TILES):
                 nc.scalar.activation(
-                    out=hs[u][:, t, :], in_=acc[u, t][:], func=ACT.Relu, bias=bias[:, t : t + 1], scale=1.0
+                    out=hs[:, t, :], in_=acc[t][:], func=ACT.Relu, bias=bias[:, t : t + 1], scale=1.0
                 )
-
-        def regroup_hs(u):
-            hs_grouped[u] = hidden_pool.tile([P, HALF, PACK], BF16, align_bytes=64, name="hs_grouped")
-            regroup(nc.vector.tensor_copy, hs_grouped[u][:], hs[u][:])
-
-        def quantise_hs(u):
-            hs_codes[u] = hidden_pool.tile([P, HALF], U32, align_bytes=64, name="hs_codes")
-            hs_scales[u] = hidden_pool.tile([P, HALF], U8, align_bytes=64, name="hs_scales")
+            hs_grouped = hidden_pool.tile([P, HALF, PACK], BF16, align_bytes=64)
+            regroup(nc.vector.tensor_copy, hs_grouped[:], hs[:])
+            hs_codes = hidden_pool.tile([P, HALF], U32, align_bytes=64)
+            hs_scales = hidden_pool.tile([P, HALF], U8, align_bytes=64)
             nc.vector.quantize_mx(
-                out=hs_codes[u][:].bitcast(FP8X4),
-                scales=hs_scales[u][:],
-                in_=hs_grouped[u][:].rearrange("p n j -> p (n j)"),
+                out=hs_codes[:].bitcast(FP8X4),
+                scales=hs_scales[:],
+                in_=hs_grouped[:].rearrange("p n j -> p (n j)"),
             )
-
-        def second_product(u):
-            scores[u] = psum_p.tile([P, HALF], F32, tag="p", name="scores")
+            scores = psum_scores.tile([P, HALF], F32, tag="scores")
             nc.tensor.matmul_mx(
-                out=scores[u][:],
+                out=scores[:],
                 lhsT=w2_codes[:].bitcast(FP8X4),
                 lhsT_scale=w2_scales[:],
-                rhs=hs_codes[u][:].bitcast(FP8X4),
-                rhs_scale=hs_scales[u][:],
+                rhs=hs_codes[:].bitcast(FP8X4),
+                rhs_scale=hs_scales[:],
                 start=True,
                 stop=True,
             )
-
-        def row_maximum(b):
-            half_max = small.tile([P, HALVES], F32)
-            for h in range(HALVES):
-                nc.vector.reduce_max(out=half_max[:, h : h + 1], in_=scores[HALVES * b + h][:], axis=AX.X)
-            neg_max[b] = small.tile([P, 1], F32, name="neg_max")
-            nc.vector.tensor_reduce(out=neg_max[b][:], in_=half_max[:], axis=AX.X, op=ALU.max, negate=True)
-
-        def kernel_matrix(b):
-            kern[b] = image_pool.tile([P, PIXELS], F32, name="kern")
-            half_sum[b] = small.tile([P, HALVES], F32, name="half_sum")
-            for h in range(HALVES):
-                nc.scalar.activation(
-                    out=kern[b][:, h * HALF : (h + 1) * HALF],
-                    in_=scores[HALVES * b + h][:],
-                    func=ACT.Exp,
-                    bias=neg_max[b][:, 0:1],
-                    scale=1.0,
-                    accum_out=half_sum[b][:, h : h + 1],
-                )
+            return scores
 
         def split(parts, values):
             nc.vector.tensor_copy(out=parts[:, :, 0], in_=values)
             nc.vector.tensor_tensor(out=parts[:, :, 1], in0=values, in1=parts[:, :, 0], op=ALU.subtract)
 
-        def split_kernel(b):
-            for part in range(2):
-                kern_parts[b, part] = image_pool.tile([P, PIXELS], BF16, name="kern_part%d" % part)
-            nc.vector.tensor_copy(out=kern_parts[b, 0][:], in_=kern[b][:])
-            nc.vector.tensor_tensor(out=kern_parts[b, 1][:], in0=kern[b][:], in1=kern_parts[b, 0][:], op=ALU.subtract)
-
-        def invert_row_sums(b, row_sum):
-            row_scale[b] = small.tile([P, 2], F32, name="row_scale")
-            nc.vector.reciprocal(out=row_scale[b][:], in_=row_sum[:])
-            row_parts[b] = small.tile([P, 2, 2], BF16, name="row_parts")
-            split(row_parts[b], row_scale[b][:])
-
-        def first_row_scale(b):
-            row_sum = small.tile([P, 2], F32)
-            nc.vector.reduce_sum(out=row_sum[:, 0:1], in_=half_sum[b][:], axis=AX.X)
-            nc.vector.memset(row_sum[:, 1:2], 1.0)
-            invert_row_sums(b, row_sum)
-            vec[b] = psum_vec.tile([P, HALF], F32, name="vec")
-
-        def flip_kernel(b, part):
-            flipped_k[b] = psum_p.tile([P, BLOCKS, P], BF16, tag="p", name="flipped_k")
-            for j in range(BLOCKS):
-                nc.tensor.transpose(flipped_k[b][:, j, :], kern_parts[b, part][:, j * P : (j + 1) * P], identity_bf16[:])
-
-        def keep_flipped(b, part):
-            kern_t_parts[b, part] = image_pool.tile([P, BLOCKS, P], BF16, name="kern_t_part%d" % part)
-            nc.scalar.copy(out=kern_t_parts[b, part][:], in_=flipped_k[b][:])
-
-        def column_sums(b):
-            sums = vec[b][:, 0 : 2 * BLOCKS].rearrange("p (j q) -> p j q", q=2)
-            nc.tensor.matmul(
-                sums,
-                lhsT=mean_of_partitions[:],
-                rhs=row_parts[b][:, 1:2, :].to_broadcast([P, BLOCKS, 2]),
-                start=True,
-                stop=False,
-            )
-            for j in range(BLOCKS):
-                for part in range(2):
-                    nc.tensor.matmul(
-                        sums[:, j, :],
-                        lhsT=kern_parts[b, part][:, j * P : (j + 1) * P],
-                        rhs=row_parts[b][:, 0, :],
-                        start=False,
-                        stop=(j == BLOCKS - 1 and part == 1),
-                    )
-
-        def column_scale(b):
-            col_sum = small.tile([P, BLOCKS], F32)
-            nc.vector.reduce_sum(
-                out=col_sum[:], in_=vec[b][:, 0 : 2 * BLOCKS].rearrange("p (j q) -> p j q", q=2), axis=AX.X
-            )
-            col_scale[b] = small.tile([P, BLOCKS], F32, name="col_scale")
-            nc.vector.reciprocal(out=col_scale[b][:], in_=col_sum[:])
-
-        def row_sums(b):
-            col_parts[b] = small.tile([P, BLOCKS, 2], BF16, name="col_parts")
-            split(col_parts[b], col_scale[b][:])
-            sums = vec[b][:, 2 * BLOCKS : 6 * BLOCKS].rearrange("p (s j q) -> p s j q", s=2, q=2)
-            for j in range(BLOCKS):
-                for part in range(2):
-                    nc.tensor.matmul(
-                        sums[:, 0, j, :],
-                        lhsT=kern_t_parts[b, part][:, j, :],
-                        rhs=col_parts[b][:, j, :],
-                        start=(part == 0),
-                        stop=(part == 1),
-                    )
-            nc.tensor.matmul(sums[:, 1, :, :], lhsT=mean_of_pixels[:], rhs=col_parts[b][:], start=True, stop=True)
-
-        def next_row_scale(b):
-            row_sum = small.tile([P, 2], F32)
-            nc.vector.reduce_sum(
-                out=row_sum[:], in_=vec[b][:, 2 * BLOCKS : 6 * BLOCKS].rearrange("p (s c) -> p s c", s=2), axis=AX.X
-            )
-            invert_row_sums(b, row_sum)
-
-        def spread(b, h):
-            for q in range(BLOCKS_PER_HALF):
-                j = h * BLOCKS_PER_HALF + q
-                nc.tensor.transpose(
-                    vec[b][:, q * P : (q + 1) * P], col_scale[b][:, j : j + 1].to_broadcast([P, P]), identity[:]
-                )
-
-        def finish(b, h):
-            if h == 0:
-                result[b] = image_pool.tile([P, PIXELS], F32, name="result")
-            cols = slice(h * HALF, (h + 1) * HALF)
-            nc.vector.scalar_tensor_tensor(
-                out=result[b][:, cols],
-                in0=kern[b][:, cols],
-                scalar=row_scale[b][:, 0:1],
-                in1=vec[b][:],
-                op0=ALU.mult,
-                op1=ALU.mult,
-            )
-            nc.sync.dma_start(out=out[b, :, cols], in_=result[b][:, cols])
-
-        def sinkhorn_start(b):
-            row_maximum(b)
-            kernel_matrix(b)
-            split_kernel(b)
-            for part in range(2):
-                flip_kernel(b, part)
-                keep_flipped(b, part)
-
-        def sinkhorn_rounds(b):
-            first_row_scale(b)
-            for r in range(ROUNDS):
-                if r > 0:
-                    row_sums(b)
-                    next_row_scale(b)
-                column_sums(b)
-                column_scale(b)
+        def sinkhorn_start(scores):
+            half_max = small.tile([P, HALVES], F32)
             for h in range(HALVES):
-                spread(b, h)
-                finish(b, h)
+                nc.vector.reduce_max(out=half_max[:, h : h + 1], in_=scores[h][:], axis=AX.X)
+            neg_top = small.tile([P, 1], F32)
+            nc.vector.tensor_reduce(out=neg_top[:], in_=half_max[:], axis=AX.X, op=ALU.max, negate=True)
+            kern = image_pool.tile([P, PIXELS], F32)
+            half_sum = small.tile([P, HALVES], F32)
+            for h in range(HALVES):
+                nc.scalar.activation(
+                    out=kern[:, h * HALF : (h + 1) * HALF],
+                    in_=scores[h][:],
+                    func=ACT.Exp,
+                    bias=neg_top[:, 0:1],
+                    scale=1.0,
+                    accum_out=half_sum[:, h : h + 1],
+                )
+            kern_hi = image_pool.tile([P, PIXELS], BF16)
+            kern_lo = image_pool.tile([P, PIXELS], BF16)
+            nc.vector.tensor_copy(out=kern_hi[:], in_=kern[:])
+            nc.vector.tensor_tensor(out=kern_lo[:], in0=kern[:], in1=kern_hi[:], op=ALU.subtract)
+            kern_parts = [kern_hi, kern_lo]
+            kern_t_parts = []
+            for part in range(PARTS):
+                flipped = psum_scores.tile([P, BLOCKS, P], BF16, tag="scores", name="flipped_k")
+                for j in range(BLOCKS):
+                    nc.tensor.transpose(flipped[:, j, :], kern_parts[part][:, j * P : (j + 1) * P], identity_bf16[:])
+                kern_t_parts.append(image_pool.tile([P, BLOCKS, P], BF16, name="kern_t_part%d" % part))
+                nc.scalar.copy(out=kern_t_parts[part][:], in_=flipped[:])
+            return kern, half_sum, kern_parts, kern_t_parts
 
-        def scores_of_half(u):
-            for g in range(PASSES):
-                s = u * PASSES + g
-                if s + LOAD_AHEAD < SLICES:
-                    load_x(s + LOAD_AHEAD)
-                regroup_x(s)
-                quantise_x(s)
-                first_product(s)
-            bias_relu(u)
-            regroup_hs(u)
-            quantise_hs(u)
-            second_product(u)
+        def sinkhorn_rounds(img, kern, half_sum, kern_parts, kern_t_parts):
+            vec = psum_vec.tile([P, HALF], F32)
+            col_sums = vec[:, 0 : PARTS * BLOCKS].rearrange("p (j part) -> p j part", part=PARTS)
+            row_sums = vec[:, PARTS * BLOCKS : 3 * PARTS * BLOCKS].rearrange(
+                "p (kind j part) -> p kind j part", kind=2, part=PARTS
+            )
+            for r in range(ROUNDS):
+                row_sum = small.tile([P, 2], F32)
+                if r == 0:
+                    nc.vector.reduce_sum(out=row_sum[:, 0:1], in_=half_sum[:], axis=AX.X)
+                    nc.vector.memset(row_sum[:, 1:2], 1.0)
+                else:
+                    col_parts = small.tile([P, BLOCKS, PARTS], BF16)
+                    split(col_parts, col_scale[:])
+                    for j in range(BLOCKS):
+                        for part in range(PARTS):
+                            nc.tensor.matmul(
+                                row_sums[:, 0, j, :],
+                                lhsT=kern_t_parts[part][:, j, :],
+                                rhs=col_parts[:, j, :],
+                                start=(part == 0),
+                                stop=(part == PARTS - 1),
+                            )
+                    nc.tensor.matmul(
+                        row_sums[:, 1, :, :], lhsT=mean_of_pixels[:], rhs=col_parts[:], start=True, stop=True
+                    )
+                    nc.vector.reduce_sum(
+                        out=row_sum[:], in_=row_sums.rearrange("p kind j part -> p kind (j part)"), axis=AX.X
+                    )
+                row_scale = small.tile([P, 2], F32)
+                nc.vector.reciprocal(out=row_scale[:], in_=row_sum[:])
+                row_parts = small.tile([P, 2, PARTS], BF16)
+                split(row_parts, row_scale[:])
+                nc.tensor.matmul(
+                    col_sums,
+                    lhsT=mean_of_partitions[:],
+                    rhs=row_parts[:, 1:2, :].to_broadcast([P, BLOCKS, PARTS]),
+                    start=True,
+                    stop=False,
+                )
+                for j in range(BLOCKS):
+                    for part in range(PARTS):
+                        nc.tensor.matmul(
+                            col_sums[:, j, :],
+                            lhsT=kern_parts[part][:, j * P : (j + 1) * P],
+                            rhs=row_parts[:, 0, :],
+                            start=False,
+                            stop=(j == BLOCKS - 1 and part == PARTS - 1),
+                        )
+                col_sum = small.tile([P, BLOCKS], F32)
+                nc.vector.reduce_sum(out=col_sum[:], in_=col_sums, axis=AX.X)
+                col_scale = small.tile([P, BLOCKS], F32)
+                nc.vector.reciprocal(out=col_scale[:], in_=col_sum[:])
+
+            result = image_pool.tile([P, PIXELS], F32)
+            for h in range(HALVES):
+                for q in range(BLOCKS_PER_HALF):
+                    j = h * BLOCKS_PER_HALF + q
+                    nc.tensor.transpose(
+                        vec[:, q * P : (q + 1) * P], col_scale[:, j : j + 1].to_broadcast([P, P]), identity[:]
+                    )
+                cols = slice(h * HALF, (h + 1) * HALF)
+                nc.vector.scalar_tensor_tensor(
+                    out=result[:, cols],
+                    in0=kern[:, cols],
+                    scalar=row_scale[:, 0:1],
+                    in1=vec[:],
+                    op0=ALU.mult,
+                    op1=ALU.mult,
+                )
+                nc.sync.dma_start(out=out[img, :, cols], in_=result[:, cols])
 
         for g in range(PASSES):
             load_x(g)
@@ -373,18 +303,14 @@ def tile_salad_pa_kernel(tc, x, Ws1, bs1, Ws2, out):
         for s in range(PASSES, LOAD_AHEAD):
             load_x(s)
         for g in range(PASSES):
-            flip_w1(g)
-            keep_w1(g)
-            quantise_w1(g)
-        flip_w2()
-        keep_w2()
-        quantise_w2()
-        widen_bias()
+            prepare_w1(g)
+        prepare_small_weights()
 
-        for b in range(IMAGES):
-            scores_of_half(b * HALVES)
-            if b > 0:
-                sinkhorn_rounds(b - 1)
-            scores_of_half(b * HALVES + 1)
-            sinkhorn_start(b)
-        sinkhorn_rounds(IMAGES - 1)
+        started = None
+        for img in range(IMAGES):
+            scores = [scores_of_half(img, 0)]
+            if img > 0:
+                sinkhorn_rounds(img - 1, *started)
+            scores.append(scores_of_half(img, 1))
+            started = sinkhorn_start(scores)
+        sinkhorn_rounds(IMAGES - 1, *started)

@@ -52,8 +52,8 @@ def tile_salad_pa_kernel(tc, x, Ws1, bs1, Ws2, out):
         grouped_pool = ctx.enter_context(tc.tile_pool(name="grouped", bufs=4))
         codes_pool = ctx.enter_context(tc.tile_pool(name="codes", bufs=3))
         hidden_pool = ctx.enter_context(tc.tile_pool(name="hidden", bufs=2))
-        image_pool = ctx.enter_context(tc.tile_pool(name="image", bufs=3))
-        small = ctx.enter_context(tc.tile_pool(name="small", bufs=4))
+        image_pool = ctx.enter_context(tc.tile_pool(name="image", bufs=IMAGES))
+        small = ctx.enter_context(tc.tile_pool(name="small", bufs=2 * IMAGES))
         psum_acc = ctx.enter_context(tc.psum_pool(name="psum_acc", bufs=HID_TILES))
         psum_scores = ctx.enter_context(tc.psum_pool(name="psum_scores", bufs=HALVES))
         psum_vec = ctx.enter_context(tc.psum_pool(name="psum_vec", bufs=2))
@@ -126,6 +126,7 @@ def tile_salad_pa_kernel(tc, x, Ws1, bs1, Ws2, out):
             )
             nc.vector.tensor_copy(out=bias[:], in_=bias_raw[:])
 
+        state = {}
         raw = {}
 
         def load_x(s):
@@ -224,73 +225,80 @@ def tile_salad_pa_kernel(tc, x, Ws1, bs1, Ws2, out):
                 nc.scalar.copy(out=kern_t_parts[part][:], in_=flipped[:])
             return kern, half_sum, kern_parts, kern_t_parts
 
-        def sinkhorn_rounds(img, kern, half_sum, kern_parts, kern_t_parts):
-            vec = psum_vec.tile([P, HALF], F32)
-            col_sums = vec[:, 0 : PARTS * BLOCKS].rearrange("p (j part) -> p j part", part=PARTS)
-            row_sums = vec[:, PARTS * BLOCKS : 3 * PARTS * BLOCKS].rearrange(
-                "p (kind j part) -> p kind j part", kind=2, part=PARTS
-            )
-            for r in range(ROUNDS):
-                row_sum = small.tile([P, 2], F32)
-                if r == 0:
-                    nc.vector.reduce_sum(out=row_sum[:, 0:1], in_=half_sum[:], axis=AX.X)
-                    nc.vector.memset(row_sum[:, 1:2], 1.0)
-                else:
-                    col_parts = small.tile([P, BLOCKS, PARTS], BF16)
-                    split(col_parts, col_scale[:])
-                    for j in range(BLOCKS):
-                        for part in range(PARTS):
-                            nc.tensor.matmul(
-                                row_sums[:, 0, j, :],
-                                lhsT=kern_t_parts[part][:, j, :],
-                                rhs=col_parts[:, j, :],
-                                start=(part == 0),
-                                stop=(part == PARTS - 1),
-                            )
-                    nc.tensor.matmul(
-                        row_sums[:, 1, :, :], lhsT=mean_of_pixels[:], rhs=col_parts[:], start=True, stop=True
-                    )
-                    nc.vector.reduce_sum(
-                        out=row_sum[:], in_=row_sums.rearrange("p kind j part -> p kind (j part)"), axis=AX.X
-                    )
-                row_scale = small.tile([P, 2], F32)
-                nc.vector.reciprocal(out=row_scale[:], in_=row_sum[:])
-                row_parts = small.tile([P, 2, PARTS], BF16)
-                split(row_parts, row_scale[:])
-                nc.tensor.matmul(
-                    col_sums,
-                    lhsT=mean_of_partitions[:],
-                    rhs=row_parts[:, 1:2, :].to_broadcast([P, BLOCKS, PARTS]),
-                    start=True,
-                    stop=False,
-                )
+        def row_step(img, r):
+            st = state[img]
+            row_sum = small.tile([P, 2], F32)
+            if r == 0:
+                nc.vector.reduce_sum(out=row_sum[:, 0:1], in_=st["half_sum"][:], axis=AX.X)
+                nc.vector.memset(row_sum[:, 1:2], 1.0)
+            else:
+                col_parts = small.tile([P, BLOCKS, PARTS], BF16)
+                split(col_parts, st["col_scale"][:])
+                row_sums = psum_vec.tile([P, 2, BLOCKS, PARTS], F32, tag="vec")
                 for j in range(BLOCKS):
                     for part in range(PARTS):
                         nc.tensor.matmul(
-                            col_sums[:, j, :],
-                            lhsT=kern_parts[part][:, j * P : (j + 1) * P],
-                            rhs=row_parts[:, 0, :],
-                            start=False,
-                            stop=(j == BLOCKS - 1 and part == PARTS - 1),
+                            row_sums[:, 0, j, :],
+                            lhsT=st["kern_t_parts"][part][:, j, :],
+                            rhs=col_parts[:, j, :],
+                            start=(part == 0),
+                            stop=(part == PARTS - 1),
                         )
-                col_sum = small.tile([P, BLOCKS], F32)
-                nc.vector.reduce_sum(out=col_sum[:], in_=col_sums, axis=AX.X)
-                col_scale = small.tile([P, BLOCKS], F32)
-                nc.vector.reciprocal(out=col_scale[:], in_=col_sum[:])
+                nc.tensor.matmul(
+                    row_sums[:, 1, :, :], lhsT=mean_of_pixels[:], rhs=col_parts[:], start=True, stop=True
+                )
+                nc.vector.reduce_sum(
+                    out=row_sum[:], in_=row_sums[:].rearrange("p kind j part -> p kind (j part)"), axis=AX.X
+                )
+            row_scale = small.tile([P, 2], F32)
+            nc.vector.reciprocal(out=row_scale[:], in_=row_sum[:])
+            st["row_scale"] = row_scale
 
+        def col_step(img):
+            st = state[img]
+            row_parts = small.tile([P, 2, PARTS], BF16)
+            split(row_parts, st["row_scale"][:])
+            col_sums = psum_vec.tile([P, BLOCKS, PARTS], F32, tag="vec")
+            nc.tensor.matmul(
+                col_sums[:],
+                lhsT=mean_of_partitions[:],
+                rhs=row_parts[:, 1:2, :].to_broadcast([P, BLOCKS, PARTS]),
+                start=True,
+                stop=False,
+            )
+            for j in range(BLOCKS):
+                for part in range(PARTS):
+                    nc.tensor.matmul(
+                        col_sums[:, j, :],
+                        lhsT=st["kern_parts"][part][:, j * P : (j + 1) * P],
+                        rhs=row_parts[:, 0, :],
+                        start=False,
+                        stop=(j == BLOCKS - 1 and part == PARTS - 1),
+                    )
+            col_sum = small.tile([P, BLOCKS], F32)
+            nc.vector.reduce_sum(out=col_sum[:], in_=col_sums[:], axis=AX.X)
+            col_scale = small.tile([P, BLOCKS], F32)
+            nc.vector.reciprocal(out=col_scale[:], in_=col_sum[:])
+            st["col_scale"] = col_scale
+
+        def finish(img):
+            st = state[img]
             result = image_pool.tile([P, PIXELS], F32)
             for h in range(HALVES):
+                spread = psum_vec.tile([P, HALF], F32, tag="vec")
                 for q in range(BLOCKS_PER_HALF):
                     j = h * BLOCKS_PER_HALF + q
                     nc.tensor.transpose(
-                        vec[:, q * P : (q + 1) * P], col_scale[:, j : j + 1].to_broadcast([P, P]), identity[:]
+                        spread[:, q * P : (q + 1) * P],
+                        st["col_scale"][:, j : j + 1].to_broadcast([P, P]),
+                        identity[:],
                     )
                 cols = slice(h * HALF, (h + 1) * HALF)
                 nc.vector.scalar_tensor_tensor(
                     out=result[:, cols],
-                    in0=kern[:, cols],
-                    scalar=row_scale[:, 0:1],
-                    in1=vec[:],
+                    in0=st["kern"][:, cols],
+                    scalar=st["row_scale"][:, 0:1],
+                    in1=spread[:],
                     op0=ALU.mult,
                     op1=ALU.mult,
                 )
@@ -306,11 +314,19 @@ def tile_salad_pa_kernel(tc, x, Ws1, bs1, Ws2, out):
             prepare_w1(g)
         prepare_small_weights()
 
-        started = None
         for img in range(IMAGES):
-            scores = [scores_of_half(img, 0)]
-            if img > 0:
-                sinkhorn_rounds(img - 1, *started)
-            scores.append(scores_of_half(img, 1))
-            started = sinkhorn_start(scores)
-        sinkhorn_rounds(IMAGES - 1, *started)
+            scores = [scores_of_half(img, h) for h in range(HALVES)]
+            kern, half_sum, kern_parts, kern_t_parts = sinkhorn_start(scores)
+            state[img] = {
+                "kern": kern,
+                "half_sum": half_sum,
+                "kern_parts": kern_parts,
+                "kern_t_parts": kern_t_parts,
+            }
+        for r in range(ROUNDS):
+            for img in range(IMAGES):
+                row_step(img, r)
+            for img in range(IMAGES):
+                col_step(img)
+        for img in range(IMAGES):
+            finish(img)

@@ -28,6 +28,7 @@ HALVES = PIXELS // HALF
 BLOCKS = PIXELS // P
 BLOCKS_PER_HALF = HALF // P
 PARTS = 2
+COPIES = 16
 SLICES = IMAGES * HALVES * PASSES
 VECTOR_COLS = 288
 LOAD_AHEAD = 6
@@ -234,22 +235,24 @@ def tile_salad_pa_kernel(tc, x, Ws1, bs1, Ws2, out):
             else:
                 col_parts = small.tile([P, BLOCKS, PARTS], BF16)
                 split(col_parts, st["col_scale"][:])
-                row_sums = psum_vec.tile([P, 2, BLOCKS, PARTS], F32, tag="vec")
+                row_sums = psum_acc.tile([P, 2, BLOCKS, COPIES, PARTS], F32, tag="acc")
                 for j in range(BLOCKS):
                     for part in range(PARTS):
                         nc.tensor.matmul(
-                            row_sums[:, 0, j, :],
+                            row_sums[:, 0, j, :, :],
                             lhsT=st["kern_t_parts"][part][:, j, :],
-                            rhs=col_parts[:, j, :],
+                            rhs=col_parts[:, j : j + 1, :].to_broadcast([P, COPIES, PARTS]),
                             start=(part == 0),
                             stop=(part == PARTS - 1),
                         )
                 nc.tensor.matmul(
-                    row_sums[:, 1, :, :], lhsT=mean_of_pixels[:], rhs=col_parts[:], start=True, stop=True
+                    row_sums[:, 1, :, :, :],
+                    lhsT=mean_of_pixels[:],
+                    rhs=col_parts[:].unsqueeze(2).to_broadcast([P, BLOCKS, COPIES, PARTS]),
+                    start=True,
+                    stop=True,
                 )
-                nc.vector.reduce_sum(
-                    out=row_sum[:], in_=row_sums[:].rearrange("p kind j part -> p kind (j part)"), axis=AX.X
-                )
+                nc.vector.tensor_reduce(out=row_sum[:], in_=row_sums[:, :, :, 0, :], axis=AX.XY, op=ALU.add)
             row_scale = small.tile([P, 2], F32)
             nc.vector.reciprocal(out=row_scale[:], in_=row_sum[:])
             st["row_scale"] = row_scale
@@ -258,25 +261,25 @@ def tile_salad_pa_kernel(tc, x, Ws1, bs1, Ws2, out):
             st = state[img]
             row_parts = small.tile([P, 2, PARTS], BF16)
             split(row_parts, st["row_scale"][:])
-            col_sums = psum_vec.tile([P, BLOCKS, PARTS], F32, tag="vec")
+            col_sums = psum_acc.tile([P, BLOCKS, COPIES, PARTS], F32, tag="acc")
             nc.tensor.matmul(
-                col_sums[:],
+                col_sums[:].rearrange("p j copy part -> p (j copy) part"),
                 lhsT=mean_of_partitions[:],
-                rhs=row_parts[:, 1:2, :].to_broadcast([P, BLOCKS, PARTS]),
+                rhs=row_parts[:, 1:2, :].to_broadcast([P, BLOCKS * COPIES, PARTS]),
                 start=True,
                 stop=False,
             )
             for j in range(BLOCKS):
                 for part in range(PARTS):
                     nc.tensor.matmul(
-                        col_sums[:, j, :],
+                        col_sums[:, j, :, :],
                         lhsT=st["kern_parts"][part][:, j * P : (j + 1) * P],
-                        rhs=row_parts[:, 0, :],
+                        rhs=row_parts[:, 0:1, :].to_broadcast([P, COPIES, PARTS]),
                         start=False,
                         stop=(j == BLOCKS - 1 and part == PARTS - 1),
                     )
             col_sum = small.tile([P, BLOCKS], F32)
-            nc.vector.reduce_sum(out=col_sum[:], in_=col_sums[:], axis=AX.X)
+            nc.vector.reduce_sum(out=col_sum[:], in_=col_sums[:, :, 0, :], axis=AX.X)
             col_scale = small.tile([P, BLOCKS], F32)
             nc.vector.reciprocal(out=col_scale[:], in_=col_sum[:])
             st["col_scale"] = col_scale

@@ -191,9 +191,11 @@ def tile_salad_pa_kernel(tc, x, Ws1, bs1, Ws2, out):
             )
             return scores
 
-        def split(parts, values):
-            nc.vector.tensor_copy(out=parts[:, :, 0], in_=values)
-            nc.vector.tensor_tensor(out=parts[:, :, 1], in0=values, in1=parts[:, :, 0], op=ALU.subtract)
+        def reciprocal_and_parts(scale, parts, sums):
+            with nc.allow_low_precision(reason="hi is meant to be the bfloat16 rounding; lo holds the rest"):
+                nc.vector.reciprocal(out=parts[:, :, 0], in_=sums)
+            nc.vector.reciprocal(out=scale, in_=sums)
+            nc.vector.tensor_tensor(out=parts[:, :, 1], in0=scale, in1=parts[:, :, 0], op=ALU.subtract)
 
         def sinkhorn_start(scores):
             half_max = small.tile([P, HALVES], F32)
@@ -233,8 +235,7 @@ def tile_salad_pa_kernel(tc, x, Ws1, bs1, Ws2, out):
                 nc.vector.reduce_sum(out=row_sum[:, 0:1], in_=st["half_sum"][:], axis=AX.X)
                 nc.vector.memset(row_sum[:, 1:2], 1.0)
             else:
-                col_parts = small.tile([P, BLOCKS, PARTS], BF16)
-                split(col_parts, st["col_scale"][:])
+                col_parts = st["col_parts"]
                 row_sums = psum_acc.tile([P, 2, BLOCKS, COPIES, PARTS], F32, tag="acc")
                 for j in range(BLOCKS):
                     for part in range(PARTS):
@@ -254,13 +255,14 @@ def tile_salad_pa_kernel(tc, x, Ws1, bs1, Ws2, out):
                 )
                 nc.vector.tensor_reduce(out=row_sum[:], in_=row_sums[:, :, :, 0, :], axis=AX.XY, op=ALU.add)
             row_scale = small.tile([P, 2], F32)
-            nc.vector.reciprocal(out=row_scale[:], in_=row_sum[:])
-            st["row_scale"] = row_scale
-
-        def col_step(img):
-            st = state[img]
             row_parts = small.tile([P, 2, PARTS], BF16)
-            split(row_parts, st["row_scale"][:])
+            reciprocal_and_parts(row_scale[:], row_parts, row_sum[:])
+            st["row_scale"] = row_scale
+            st["row_parts"] = row_parts
+
+        def col_step(img, r):
+            st = state[img]
+            row_parts = st["row_parts"]
             col_sums = psum_acc.tile([P, BLOCKS, COPIES, PARTS], F32, tag="acc")
             nc.tensor.matmul(
                 col_sums[:].rearrange("p j copy part -> p (j copy) part"),
@@ -281,7 +283,12 @@ def tile_salad_pa_kernel(tc, x, Ws1, bs1, Ws2, out):
             col_sum = small.tile([P, BLOCKS], F32)
             nc.vector.reduce_sum(out=col_sum[:], in_=col_sums[:, :, 0, :], axis=AX.X)
             col_scale = small.tile([P, BLOCKS], F32)
-            nc.vector.reciprocal(out=col_scale[:], in_=col_sum[:])
+            if r < ROUNDS - 1:
+                col_parts = small.tile([P, BLOCKS, PARTS], BF16)
+                reciprocal_and_parts(col_scale[:], col_parts, col_sum[:])
+                st["col_parts"] = col_parts
+            else:
+                nc.vector.reciprocal(out=col_scale[:], in_=col_sum[:])
             st["col_scale"] = col_scale
 
         def finish(img):
@@ -326,10 +333,18 @@ def tile_salad_pa_kernel(tc, x, Ws1, bs1, Ws2, out):
                 "kern_parts": kern_parts,
                 "kern_t_parts": kern_t_parts,
             }
-        for r in range(ROUNDS):
-            for img in range(IMAGES):
-                row_step(img, r)
-            for img in range(IMAGES):
-                col_step(img)
-        for img in range(IMAGES):
-            finish(img)
+        last = IMAGES - 1
+        for r in range(ROUNDS + 1):
+            if r > 0:
+                row_step(last, r - 1)
+            for img in range(last):
+                if r < ROUNDS:
+                    row_step(img, r)
+            if r > 0:
+                col_step(last, r - 1)
+            for img in range(last):
+                if r < ROUNDS:
+                    col_step(img, r)
+                else:
+                    finish(img)
+        finish(last)

@@ -333,18 +333,12 @@ def tile_salad_pa_kernel(tc, x, Ws1, bs1, Ws2, out):
                 "kern_parts": kern_parts,
                 "kern_t_parts": kern_t_parts,
             }
-        last = IMAGES - 1
-        for r in range(ROUNDS + 1):
-            if r > 0:
-                row_step(last, r - 1)
-            for img in range(last):
-                if r < ROUNDS:
+        for turn in range(2 * ROUNDS + IMAGES):
+            for img in reversed(range(IMAGES)):
+                r, second = divmod(turn - img, 2)
+                if 0 <= r < ROUNDS and second == 0:
                     row_step(img, r)
-            if r > 0:
-                col_step(last, r - 1)
-            for img in range(last):
-                if r < ROUNDS:
+                if 0 <= r < ROUNDS and second == 1:
                     col_step(img, r)
-                else:
+                if r == ROUNDS and second == 0:
                     finish(img)
-        finish(last)

@@ -197,7 +197,7 @@ def tile_salad_pa_kernel(tc, x, Ws1, bs1, Ws2, out):
             nc.vector.reciprocal(out=scale, in_=sums)
             nc.vector.tensor_tensor(out=parts[:, :, 1], in0=scale, in1=parts[:, :, 0], op=ALU.subtract)
 
-        def sinkhorn_start(scores):
+        def sinkhorn_start(scores, pieces):
             half_max = small.tile([P, HALVES], F32)
             for h in range(HALVES):
                 nc.vector.reduce_max(out=half_max[:, h : h + 1], in_=scores[h][:], axis=AX.X)
@@ -216,16 +216,25 @@ def tile_salad_pa_kernel(tc, x, Ws1, bs1, Ws2, out):
                 )
             kern_hi = image_pool.tile([P, PIXELS], BF16)
             kern_lo = image_pool.tile([P, PIXELS], BF16)
-            nc.vector.tensor_copy(out=kern_hi[:], in_=kern[:])
-            nc.vector.tensor_tensor(out=kern_lo[:], in0=kern[:], in1=kern_hi[:], op=ALU.subtract)
             kern_parts = [kern_hi, kern_lo]
-            kern_t_parts = []
-            for part in range(PARTS):
-                flipped = psum_scores.tile([P, BLOCKS, P], BF16, tag="scores", name="flipped_k")
-                for j in range(BLOCKS):
-                    nc.tensor.transpose(flipped[:, j, :], kern_parts[part][:, j * P : (j + 1) * P], identity_bf16[:])
-                kern_t_parts.append(image_pool.tile([P, BLOCKS, P], BF16, name="kern_t_part%d" % part))
-                nc.scalar.copy(out=kern_t_parts[part][:], in_=flipped[:])
+            kern_t_parts = [
+                image_pool.tile([P, BLOCKS, P], BF16, name="kern_t_part%d" % part) for part in range(PARTS)
+            ]
+            blocks = BLOCKS // pieces
+            for piece in range(pieces):
+                cols = slice(piece * blocks * P, (piece + 1) * blocks * P)
+                nc.vector.tensor_copy(out=kern_hi[:, cols], in_=kern[:, cols])
+                nc.vector.tensor_tensor(out=kern_lo[:, cols], in0=kern[:, cols], in1=kern_hi[:, cols], op=ALU.subtract)
+                for part in range(PARTS):
+                    flipped = psum_scores.tile([P, blocks, P], BF16, tag="scores", name="flipped_k")
+                    for q in range(blocks):
+                        j = piece * blocks + q
+                        nc.tensor.transpose(
+                            flipped[:, q, :], kern_parts[part][:, j * P : (j + 1) * P], identity_bf16[:]
+                        )
+                    nc.scalar.copy(
+                        out=kern_t_parts[part][:, piece * blocks : (piece + 1) * blocks, :], in_=flipped[:]
+                    )
             return kern, half_sum, kern_parts, kern_t_parts
 
         def row_step(img, r):
@@ -326,7 +335,7 @@ def tile_salad_pa_kernel(tc, x, Ws1, bs1, Ws2, out):
 
         for img in range(IMAGES):
             scores = [scores_of_half(img, h) for h in range(HALVES)]
-            kern, half_sum, kern_parts, kern_t_parts = sinkhorn_start(scores)
+            kern, half_sum, kern_parts, kern_t_parts = sinkhorn_start(scores, HALVES if img == IMAGES - 1 else 1)
             state[img] = {
                 "kern": kern,
                 "half_sum": half_sum,

@@ -323,12 +323,12 @@ def tile_salad_pa_kernel(tc, x, Ws1, bs1, Ws2, out):
                 )
                 nc.sync.dma_start(out=out[img, :, cols], in_=result[:, cols])
 
-        for g in range(PASSES):
-            load_x(g)
-            load_w1(g)
-        load_small_weights()
-        for s in range(PASSES, LOAD_AHEAD):
+        for s in range(PASSES):
             load_x(s)
+        for g in range(PASSES):
+            load_w1(g)
+            load_x(PASSES + g)
+        load_small_weights()
         for g in range(PASSES):
             prepare_w1(g)
         prepare_small_weights()

@@ -81,12 +81,8 @@ def tile_salad_pa_kernel(tc, x, Ws1, bs1, Ws2, out):
         w2_codes = const.tile([P, CLUSTERS], U32, align_bytes=64)
         w2_scales = const.tile([P, CLUSTERS], U8, align_bytes=64)
 
-        def load_w1(g):
-            cols = slice(g * K_PASS, (g + 1) * K_PASS)
-            nc.sync.dma_start(
-                out=w1_raw[:].rearrange("m (t c) -> m t c", t=HID_TILES)[:, :, cols],
-                in_=Ws1.rearrange("(m t) c -> m t c", t=HID_TILES)[:, :, cols],
-            )
+        def load_w1():
+            nc.sync.dma_start(out=w1_raw[:], in_=Ws1.rearrange("(m t) c -> m (t c)", t=HID_TILES))
 
         def load_small_weights():
             nc.sync.dma_start(out=w2_raw[:], in_=Ws2)
@@ -325,10 +321,10 @@ def tile_salad_pa_kernel(tc, x, Ws1, bs1, Ws2, out):
 
         for s in range(PASSES):
             load_x(s)
-        for g in range(PASSES):
-            load_w1(g)
-            load_x(PASSES + g)
+        load_w1()
         load_small_weights()
+        for s in range(PASSES, LOAD_AHEAD):
+            load_x(s)
         for g in range(PASSES):
             prepare_w1(g)
         prepare_small_weights()

@@ -252,11 +252,7 @@ def tile_salad_pa_kernel(tc, x, Ws1, bs1, Ws2, out):
                             stop=(part == PARTS - 1),
                         )
                 nc.tensor.matmul(
-                    row_sums[:, 1, :, :, :],
-                    lhsT=mean_of_pixels[:],
-                    rhs=col_parts[:].unsqueeze(2).to_broadcast([P, BLOCKS, COPIES, PARTS]),
-                    start=True,
-                    stop=True,
+                    row_sums[:, 1, :, 0, :], lhsT=mean_of_pixels[:], rhs=col_parts[:], start=True, stop=True
                 )
                 nc.vector.tensor_reduce(out=row_sum[:], in_=row_sums[:, :, :, 0, :], axis=AX.XY, op=ALU.add)
             row_scale = small.tile([P, 2], F32)
@@ -269,22 +265,22 @@ def tile_salad_pa_kernel(tc, x, Ws1, bs1, Ws2, out):
             st = state[img]
             row_parts = st["row_parts"]
             col_sums = psum_acc.tile([P, BLOCKS, COPIES, PARTS], F32, tag="acc")
-            nc.tensor.matmul(
-                col_sums[:].rearrange("p j copy part -> p (j copy) part"),
-                lhsT=mean_of_partitions[:],
-                rhs=row_parts[:, 1:2, :].to_broadcast([P, BLOCKS * COPIES, PARTS]),
-                start=True,
-                stop=False,
-            )
-            for j in range(BLOCKS):
-                for part in range(PARTS):
+            for part in range(PARTS):
+                for j in range(BLOCKS):
                     nc.tensor.matmul(
                         col_sums[:, j, :, :],
                         lhsT=st["kern_parts"][part][:, j * P : (j + 1) * P],
                         rhs=row_parts[:, 0:1, :].to_broadcast([P, COPIES, PARTS]),
-                        start=False,
-                        stop=(j == BLOCKS - 1 and part == PARTS - 1),
+                        start=(part == 0 and j == 0),
+                        stop=False,
                     )
+            nc.tensor.matmul(
+                col_sums[:, :, 0, :],
+                lhsT=mean_of_partitions[:],
+                rhs=row_parts[:, 1:2, :].to_broadcast([P, BLOCKS, PARTS]),
+                start=False,
+                stop=True,
+            )
             col_sum = small.tile([P, BLOCKS], F32)
             nc.vector.reduce_sum(out=col_sum[:], in_=col_sums[:, :, 0, :], axis=AX.X)
             col_scale = small.tile([P, BLOCKS], F32)

from contextlib import ExitStack

import concourse.mybir as mybir
from concourse.masks import make_identity

F32 = mybir.dt.float32
BF16 = mybir.dt.bfloat16
U32 = mybir.dt.uint32
U8 = mybir.dt.uint8
FP8X4 = mybir.dt.float8_e4m3fn_x4
ACT = mybir.ActivationFunctionType
ALU = mybir.AluOpType
AX = mybir.AxisListType

P = 128
PACK = 4
K_PASS = P * PACK
IMAGES = 4
CHANNELS = 1536
PIXELS = 1024
HIDDEN = 512
CLUSTERS = 128
ROUNDS = 3
PASSES = CHANNELS // K_PASS
HID_TILES = HIDDEN // P
HALF = 512
HALVES = PIXELS // HALF
BLOCKS = PIXELS // P
BLOCKS_PER_HALF = HALF // P
PARTS = 2
COPIES = 16
SLICES = IMAGES * HALVES * PASSES
VECTOR_COLS = 288
LOAD_AHEAD = 6

FLOPS = 2 * IMAGES * PIXELS * (HIDDEN * CHANNELS + CLUSTERS * HIDDEN)


def regroup(copy, grouped, rows):
    copy(
        out=grouped.rearrange("p (run n) j -> p run j n", n=4),
        in_=rows.rearrange("p j (run n) -> p run j n", n=4),
    )


def tile_salad_pa_kernel(tc, x, Ws1, bs1, Ws2, out):
    nc = tc.nc
    pixels_of = x.rearrange("img c row col -> img c (row col)")

    with ExitStack() as ctx:
        const = ctx.enter_context(tc.tile_pool(name="const", bufs=1))
        raw_pool = ctx.enter_context(tc.tile_pool(name="raw", bufs=LOAD_AHEAD + 2))
        grouped_pool = ctx.enter_context(tc.tile_pool(name="grouped", bufs=4))
        codes_pool = ctx.enter_context(tc.tile_pool(name="codes", bufs=3))
        hidden_pool = ctx.enter_context(tc.tile_pool(name="hidden", bufs=2))
        image_pool = ctx.enter_context(tc.tile_pool(name="image", bufs=IMAGES))
        small = ctx.enter_context(tc.tile_pool(name="small", bufs=2 * IMAGES))
        psum_acc = ctx.enter_context(tc.psum_pool(name="psum_acc", bufs=HID_TILES))
        psum_scores = ctx.enter_context(tc.psum_pool(name="psum_scores", bufs=HALVES))
        psum_vec = ctx.enter_context(tc.psum_pool(name="psum_vec", bufs=2))

        identity = const.tile([P, P], F32)
        make_identity(nc, identity[:])
        identity_bf16 = const.tile([P, P], BF16)
        make_identity(nc, identity_bf16[:])
        mean_of_pixels = const.tile([P, P], BF16)
        nc.vector.memset(mean_of_pixels[:], 1.0 / PIXELS)
        mean_of_partitions = const.tile([P, P], BF16)
        nc.vector.memset(mean_of_partitions[:], 1.0 / P)

        w1_raw = const.tile([P, HID_TILES * CHANNELS], BF16)
        w2_raw = const.tile([P, HIDDEN], BF16)
        bias_raw = const.tile([P, HID_TILES], BF16)
        bias = const.tile([P, HID_TILES], F32)
        w1_words = w1_raw[:].bitcast(F32).rearrange("m (t g p w) -> m t g w p", t=HID_TILES, g=PASSES, w=2)
        w2_words = w2_raw[:].bitcast(F32).rearrange("m (p w) -> m w p", w=2)
        w1_grouped = const.tile([P, PASSES, HIDDEN, 2], F32, align_bytes=64)
        w1_codes = const.tile([P, PASSES, HIDDEN], U32, align_bytes=64)
        w1_scales = const.tile([P, PASSES, HIDDEN], U8, align_bytes=64)
        w2_grouped = const.tile([P, CLUSTERS, 2], F32, align_bytes=64)
        w2_codes = const.tile([P, CLUSTERS], U32, align_bytes=64)
        w2_scales = const.tile([P, CLUSTERS], U8, align_bytes=64)

        def load_w1():
            nc.sync.dma_start(out=w1_raw[:], in_=Ws1.rearrange("(m t) c -> m (t c)", t=HID_TILES))

        def load_small_weights():
            nc.sync.dma_start(out=w2_raw[:], in_=Ws2)
            with nc.allow_non_contiguous_dma(reason="512 bias values, 4 to a partition"):
                nc.sync.dma_start(out=bias_raw[:], in_=bs1.rearrange("(m t) -> m t", t=HID_TILES))

        def prepare_w1(g):
            flipped = []
            for pair in range(HID_TILES // 2):
                flipped.append(psum_scores.tile([P, 2, 2, P], F32, tag="scores", name="flipped_w"))
                for member in range(2):
                    for w in range(2):
                        nc.tensor.transpose(
                            flipped[pair][:, member, w, :], w1_words[:, 2 * pair + member, g, w, :], identity[:]
                        )
            for pair in range(HID_TILES // 2):
                nc.scalar.copy(
                    out=w1_grouped[:, g, 2 * pair * P : (2 * pair + 2) * P, :].rearrange(
                        "p (member m) w -> p member m w", member=2
                    ),
                    in_=flipped[pair][:].rearrange("p member w m -> p member m w"),
                )
            nc.vector.quantize_mx(
                out=w1_codes[:, g, :].bitcast(FP8X4),
                scales=w1_scales[:, g, :],
                in_=w1_grouped[:, g, :, :].rearrange("p m w -> p (m w)").bitcast(BF16),
            )

        def prepare_small_weights():
            flipped = psum_scores.tile([P, 2, P], F32, tag="scores", name="flipped_w")
            for w in range(2):
                nc.tensor.transpose(flipped[:, w, :], w2_words[:, w, :], identity[:])
            nc.scalar.copy(out=w2_grouped[:], in_=flipped[:].rearrange("p w m -> p m w"))
            nc.vector.quantize_mx(
                out=w2_codes[:].bitcast(FP8X4),
                scales=w2_scales[:],
                in_=w2_grouped[:].rearrange("p m w -> p (m w)").bitcast(BF16),
            )
            nc.vector.tensor_copy(out=bias[:], in_=bias_raw[:])

        state = {}
        raw = {}

        def load_x(s):
            img, rest = divmod(s, HALVES * PASSES)
            h, g = divmod(rest, PASSES)
            raw[s] = raw_pool.tile([P, PACK, HALF], BF16, name="raw")
            rows = pixels_of[img, g * K_PASS : (g + 1) * K_PASS, h * HALF : (h + 1) * HALF]
            nc.sync.dma_start(out=raw[s][:], in_=rows.rearrange("(p j) n -> p j n", j=PACK))

        def scores_of_half(img, h):
            x_codes = codes_pool.tile([P, PASSES, HALF], U32, align_bytes=64)
            x_scales = codes_pool.tile([P, PASSES, HALF], U8, align_bytes=64)
            acc = []
            for g in range(PASSES):
                s = (img * HALVES + h) * PASSES + g
                if s + LOAD_AHEAD < SLICES:
                    load_x(s + LOAD_AHEAD)
                x_grouped = grouped_pool.tile([P, HALF, PACK], BF16, align_bytes=64)
                regroup(nc.vector.tensor_copy, x_grouped[:, :VECTOR_COLS, :], raw[s][:, :, :VECTOR_COLS])
                regroup(nc.scalar.copy, x_grouped[:, VECTOR_COLS:, :], raw[s][:, :, VECTOR_COLS:])
                nc.vector.quantize_mx(
                    out=x_codes[:, g, :].bitcast(FP8X4),
                    scales=x_scales[:, g, :],
                    in_=x_grouped[:].rearrange("p n j -> p (n j)"),
                )
                for t in range(HID_TILES):
                    if g == 0:
                        acc.append(psum_acc.tile([P, HALF], F32, name="acc"))
                    nc.tensor.matmul_mx(
                        out=acc[t][:],
                        lhsT=w1_codes[:, g, t * P : (t + 1) * P].bitcast(FP8X4),
                        lhsT_scale=w1_scales[:, g, t * P : (t + 1) * P],
                        rhs=x_codes[:, g, :].bitcast(FP8X4),
                        rhs_scale=x_scales[:, g, :],
                        start=(g == 0),
                        stop=(g == PASSES - 1),
                    )
            hs = hidden_pool.tile([P, HID_TILES, HALF], BF16)
            for t in range(HID_TILES):
                nc.scalar.activation(
                    out=hs[:, t, :], in_=acc[t][:], func=ACT.Relu, bias=bias[:, t : t + 1], scale=1.0
                )
            hs_grouped = hidden_pool.tile([P, HALF, PACK], BF16, align_bytes=64)
            regroup(nc.vector.tensor_copy, hs_grouped[:], hs[:])
            hs_codes = hidden_pool.tile([P, HALF], U32, align_bytes=64)
            hs_scales = hidden_pool.tile([P, HALF], U8, align_bytes=64)
            nc.vector.quantize_mx(
                out=hs_codes[:].bitcast(FP8X4),
                scales=hs_scales[:],
                in_=hs_grouped[:].rearrange("p n j -> p (n j)"),
            )
            scores = psum_scores.tile([P, HALF], F32, tag="scores")
            nc.tensor.matmul_mx(
                out=scores[:],
                lhsT=w2_codes[:].bitcast(FP8X4),
                lhsT_scale=w2_scales[:],
                rhs=hs_codes[:].bitcast(FP8X4),
                rhs_scale=hs_scales[:],
                start=True,
                stop=True,
            )
            return scores

        def reciprocal_and_parts(scale, parts, sums):
            with nc.allow_low_precision(reason="hi is meant to be the bfloat16 rounding; lo holds the rest"):
                nc.vector.reciprocal(out=parts[:, :, 0], in_=sums)
            nc.vector.reciprocal(out=scale, in_=sums)
            nc.vector.tensor_tensor(out=parts[:, :, 1], in0=scale, in1=parts[:, :, 0], op=ALU.subtract)

        def sinkhorn_start(scores, pieces):
            half_max = small.tile([P, HALVES], F32)
            for h in range(HALVES):
                nc.vector.reduce_max(out=half_max[:, h : h + 1], in_=scores[h][:], axis=AX.X)
            neg_top = small.tile([P, 1], F32)
            nc.vector.tensor_reduce(out=neg_top[:], in_=half_max[:], axis=AX.X, op=ALU.max, negate=True)
            kern = image_pool.tile([P, PIXELS], F32)
            half_sum = small.tile([P, HALVES], F32)
            for h in range(HALVES):
                nc.scalar.activation(
                    out=kern[:, h * HALF : (h + 1) * HALF],
                    in_=scores[h][:],
                    func=ACT.Exp,
                    bias=neg_top[:, 0:1],
                    scale=1.0,
                    accum_out=half_sum[:, h : h + 1],
                )
            kern_hi = image_pool.tile([P, PIXELS], BF16)
            kern_lo = image_pool.tile([P, PIXELS], BF16)
            kern_parts = [kern_hi, kern_lo]
            kern_t_parts = [
                image_pool.tile([P, BLOCKS, P], BF16, name="kern_t_part%d" % part) for part in range(PARTS)
            ]
            blocks = BLOCKS // pieces
            for piece in range(pieces):
                cols = slice(piece * blocks * P, (piece + 1) * blocks * P)
                nc.vector.tensor_copy(out=kern_hi[:, cols], in_=kern[:, cols])
                nc.vector.tensor_tensor(out=kern_lo[:, cols], in0=kern[:, cols], in1=kern_hi[:, cols], op=ALU.subtract)
                for part in range(PARTS):
                    flipped = psum_scores.tile([P, blocks, P], BF16, tag="scores", name="flipped_k")
                    for q in range(blocks):
                        j = piece * blocks + q
                        nc.tensor.transpose(
                            flipped[:, q, :], kern_parts[part][:, j * P : (j + 1) * P], identity_bf16[:]
                        )
                    nc.scalar.copy(
                        out=kern_t_parts[part][:, piece * blocks : (piece + 1) * blocks, :], in_=flipped[:]
                    )
            return kern, half_sum, kern_parts, kern_t_parts

        def row_step(img, r):
            st = state[img]
            row_sum = small.tile([P, 2], F32)
            if r == 0:
                nc.vector.reduce_sum(out=row_sum[:, 0:1], in_=st["half_sum"][:], axis=AX.X)
                nc.vector.memset(row_sum[:, 1:2], 1.0)
            else:
                col_parts = st["col_parts"]
                row_sums = psum_acc.tile([P, 2, BLOCKS, COPIES, PARTS], F32, tag="acc")
                for j in range(BLOCKS):
                    for part in range(PARTS):
                        nc.tensor.matmul(
                            row_sums[:, 0, j, :, :],
                            lhsT=st["kern_t_parts"][part][:, j, :],
                            rhs=col_parts[:, j : j + 1, :].to_broadcast([P, COPIES, PARTS]),
                            start=(part == 0),
                            stop=(part == PARTS - 1),
                        )
                nc.tensor.matmul(
                    row_sums[:, 1, :, 0, :], lhsT=mean_of_pixels[:], rhs=col_parts[:], start=True, stop=True
                )
                nc.vector.tensor_reduce(out=row_sum[:], in_=row_sums[:, :, :, 0, :], axis=AX.XY, op=ALU.add)
            row_scale = small.tile([P, 2], F32)
            row_parts = small.tile([P, 2, PARTS], BF16)
            reciprocal_and_parts(row_scale[:], row_parts, row_sum[:])
            st["row_scale"] = row_scale
            st["row_parts"] = row_parts

        def col_step(img, r):
            st = state[img]
            row_parts = st["row_parts"]
            col_sums = psum_acc.tile([P, BLOCKS, COPIES, PARTS], F32, tag="acc")
            for part in range(PARTS):
                for j in range(BLOCKS):
                    nc.tensor.matmul(
                        col_sums[:, j, :, :],
                        lhsT=st["kern_parts"][part][:, j * P : (j + 1) * P],
                        rhs=row_parts[:, 0:1, :].to_broadcast([P, COPIES, PARTS]),
                        start=(part == 0 and j == 0),
                        stop=False,
                    )
            nc.tensor.matmul(
                col_sums[:, :, 0, :],
                lhsT=mean_of_partitions[:],
                rhs=row_parts[:, 1:2, :].to_broadcast([P, BLOCKS, PARTS]),
                start=False,
                stop=True,
            )
            col_sum = small.tile([P, BLOCKS], F32)
            nc.vector.reduce_sum(out=col_sum[:], in_=col_sums[:, :, 0, :], axis=AX.X)
            col_scale = small.tile([P, BLOCKS], F32)
            if r < ROUNDS - 1:
                col_parts = small.tile([P, BLOCKS, PARTS], BF16)
                reciprocal_and_parts(col_scale[:], col_parts, col_sum[:])
                st["col_parts"] = col_parts
            else:
                nc.vector.reciprocal(out=col_scale[:], in_=col_sum[:])
            st["col_scale"] = col_scale

        def finish(img):
            st = state[img]
            result = image_pool.tile([P, PIXELS], F32)
            for h in range(HALVES):
                spread = psum_vec.tile([P, HALF], F32, tag="vec")
                for q in range(BLOCKS_PER_HALF):
                    j = h * BLOCKS_PER_HALF + q
                    nc.tensor.transpose(
                        spread[:, q * P : (q + 1) * P],
                        st["col_scale"][:, j : j + 1].to_broadcast([P, P]),
                        identity[:],
                    )
                cols = slice(h * HALF, (h + 1) * HALF)
                nc.vector.scalar_tensor_tensor(
                    out=result[:, cols],
                    in0=st["kern"][:, cols],
                    scalar=st["row_scale"][:, 0:1],
                    in1=spread[:],
                    op0=ALU.mult,
                    op1=ALU.mult,
                )
                nc.sync.dma_start(out=out[img, :, cols], in_=result[:, cols])

        for s in range(PASSES):
            load_x(s)
        load_w1()
        load_small_weights()
        for s in range(PASSES, LOAD_AHEAD):
            load_x(s)
        for g in range(PASSES):
            prepare_w1(g)
        prepare_small_weights()

        for img in range(IMAGES):
            scores = [scores_of_half(img, h) for h in range(HALVES)]
            kern, half_sum, kern_parts, kern_t_parts = sinkhorn_start(scores, HALVES if img == IMAGES - 1 else 1)
            state[img] = {
                "kern": kern,
                "half_sum": half_sum,
                "kern_parts": kern_parts,
                "kern_t_parts": kern_t_parts,
            }
        for turn in range(2 * ROUNDS + IMAGES):
            for img in reversed(range(IMAGES)):
                r, second = divmod(turn - img, 2)
                if 0 <= r < ROUNDS and second == 0:
                    row_step(img, r)
                if 0 <= r < ROUNDS and second == 1:
                    col_step(img, r)
                if r == ROUNDS and second == 0:
                    finish(img)
